import numpy as np
import ml_dtypes


def mxq(x, axis, fmt="e4m3"):
    dtype, down = {"e4m3": (ml_dtypes.float8_e4m3fn, 7), "e5m2": (ml_dtypes.float8_e5m2, 14)}[fmt]
    v = np.moveaxis(np.asarray(x, np.float32).astype(ml_dtypes.bfloat16).astype(np.float64), axis, -1)
    blocks = v.reshape(v.shape[:-1] + (-1, 32))
    amax = np.abs(blocks).max(-1, keepdims=True)
    byte = np.maximum(np.where(amax > 0, np.frexp(amax)[1] - 1 + 127, 0) - down, 1)
    scale = np.exp2(byte - 127.0)
    codes = (blocks / scale).astype(np.float32).astype(dtype).astype(np.float64)
    return np.moveaxis((codes * scale).reshape(v.shape), -1, axis)


WIDE = False


def mx_kscale(k):
    if not WIDE:
        return np.ones(k)
    levels = np.array([10, -10, 5, -5, 0])
    a = np.random.permutation(np.resize(levels, k // 512 * 4)).reshape(k // 512, 4)
    idx = np.arange(k)
    return np.exp2(a[idx // 512, idx % 128 // 32])


BF16 = ml_dtypes.bfloat16


def bf(x):
    return np.asarray(x, np.float32).astype(BF16)


def f64(x):
    return np.asarray(x).astype(np.float64)


E2M1 = np.array([0.0, 0.5, 1.0, 1.5, 2.0, 3.0, 4.0, 6.0, -0.0, -0.5, -1.0, -1.5, -2.0, -3.0, -4.0, -6.0])


def pack_weight(w, fmt):
    k, n = w.shape
    w = f64(bf(w)).reshape(k // 32, 32, n)
    amax = np.abs(w).max(1)
    if fmt == "e4m3":
        byte = np.frexp(amax)[1] - 1 + 127 - 7
    else:
        mant, ex = np.frexp(amax / 6.0)
        byte = np.where(mant > 0.5, ex, ex - 1) + 127
    byte = np.clip(np.where(amax > 0, byte, 1), 1, 254)
    scaled = (w * np.exp2(127.0 - byte)[:, None, :]).reshape(k, n).astype(np.float32)
    by_word = np.ascontiguousarray(scaled.reshape(k // 512, 128, 4, n).transpose(0, 1, 3, 2))
    if fmt == "e4m3":
        words = by_word.astype(ml_dtypes.float8_e4m3fn).view(np.uint8)
    else:
        c = by_word.astype(ml_dtypes.float4_e2m1fn).view(np.uint8) & 0xF
        words = c[..., 0::2] | (c[..., 1::2] << 4)
    return np.ascontiguousarray(words), np.ascontiguousarray(byte.astype(np.uint8).reshape(k // 512, 16, n))


def unpack_weight(words, scales, fmt):
    g, p, n, _ = words.shape
    if fmt == "e4m3":
        vals = np.ascontiguousarray(words).view(ml_dtypes.float8_e4m3fn).astype(np.float64)
    else:
        nib = np.empty((g, p, n, 4), np.uint8)
        nib[..., 0::2] = words & 0xF
        nib[..., 1::2] = words >> 4
        vals = E2M1[nib]
    vals = vals * np.repeat(np.exp2(scales.astype(np.float64) - 127.0), 8, axis=1)[..., None]
    return vals.transpose(0, 1, 3, 2).reshape(g * 512, n)

def pack4(w):
    words, scales = pack_weight(w, "e2m1")
    return words.reshape(words.shape[0], 128, -1), scales


def unpack4(words, scales):
    return unpack_weight(words.reshape(words.shape[0], 128, -1, 2), scales, "e2m1")


B, T, D, NH, HD, G, RD, F = 1, 640, 1024, 8, 128, 2, 16, 4096
HKV = NH // G
C = NH * HD


def setup_inputs():
    s = mx_kscale(C).reshape(NH, HD)
    sh = np.where(np.arange(NH) % 2 == 0, s.max(axis=1), s.min(axis=1))
    v = np.random.standard_normal((B, HKV, T, HD))
    a = 0.4 * np.random.standard_normal((B, HKV, G, T, HD)) + 0.4 * v[:, :, None]
    x = bf(np.random.standard_normal((B, T, D)) * np.random.uniform(0.5, 2.0, (B, T, 1)))
    wo = np.random.standard_normal((D, C)) / np.sqrt(C) / np.repeat(sh, HD)[None, :]
    wo_words, wo_scales = pack4(np.ascontiguousarray(wo.T))
    return {"attn_out": bf(a * sh.reshape(HKV, G)[None, :, :, None, None]),
            "v": bf(v),
            "x": x,
            "wo_words": wo_words,
            "wo_scales": wo_scales,
            "attn_scale": bf(1.0 + 0.1 * np.random.standard_normal(D))}


def reference(attn_out, v, x, wo_words, wo_scales, attn_scale):
    y_g = f64(attn_out).transpose(0, 3, 1, 2, 4)
    v_t = f64(v).transpose(0, 2, 1, 3)
    vn = v_t / np.maximum(np.sqrt(np.sum(np.square(v_t), axis=-1, keepdims=True)), 1e-12)
    vn = vn[:, :, :, None, :]
    proj = np.sum(y_g * vn, axis=-1, keepdims=True) * vn
    y = (y_g - proj).reshape(B, T, C)
    return f64(x) + f64(attn_scale) * (mxq(y, 2, "e4m3") @ unpack4(wo_words, wo_scales))

@@ -1,0 +1,252 @@
+from contextlib import ExitStack
+
+import concourse.mybir as mybir
+from concourse.masks import make_identity
+
+BF16 = mybir.dt.bfloat16
+F32 = mybir.dt.float32
+I32 = mybir.dt.int32
+U32 = mybir.dt.uint32
+U8 = mybir.dt.uint8
+FP8X4 = mybir.dt.float8_e4m3fn_x4
+FP4X4 = mybir.dt.float4_e2m1fn_x4
+ALU = mybir.AluOpType
+ACT = mybir.ActivationFunctionType
+
+P = 128
+TOKENS = 640
+TILES = TOKENS // P
+KV_HEADS = 4
+GROUP = 2
+HEADS = KV_HEADS * GROUP
+HD = 128
+C = HEADS * HD
+D = 1024
+PACK = 4
+K_PASS = P * PACK
+PASSES = C // K_PASS
+N_TILES = D // P
+BANK = 512
+HALVES = D // BANK
+MIN_NORM = 1e-12
+
+FLOPS = 2 * TOKENS * C * D
+
+
+def tile_block_pb_kernel(tc, attn_out, v, x, wo_words, wo_scales, attn_scale, out):
+    nc = tc.nc
+    a_rows = attn_out.rearrange("b h g t d -> t (b h g) d")
+    v_rows = v.rearrange("b h t d -> t (b h) d")
+    x_rows = x.rearrange("b t n -> (b t) n")
+    out_rows = out.rearrange("b t n -> (b t) n")
+
+    with ExitStack() as ctx:
+        consts = ctx.enter_context(tc.tile_pool(name="consts", bufs=1))
+        per_tile = ctx.enter_context(tc.tile_pool(name="per_tile", bufs=TILES))
+        turn_psum = ctx.enter_context(tc.psum_pool(name="turn_psum", bufs=2))
+        acc_psum = ctx.enter_context(tc.psum_pool(name="acc_psum", bufs=2))
+        back_psum = ctx.enter_context(tc.psum_pool(name="back_psum", bufs=4))
+        ctx.enter_context(tc.manual_schedule())
+
+        a_tiles, v_tiles, x_tiles = [], [], []
+        sumsq_tiles, dot_tiles, coef_tiles = [], [], []
+        y_tiles, grouped_tiles, code_tiles, plane_tiles = [], [], [], []
+        scaled_tiles, back_tiles = [], []
+
+        ident = consts.tile([P, P], F32)
+        make_identity(nc, ident[:])
+        gain_rows = consts.tile([P, P], BF16)
+        nc.gpsimd.memset(gain_rows[:], 0.0)
+        w_planes = consts.tile([P, PASSES, D], U8, align_bytes=64)
+        nc.vector.memset(w_planes[:].bitcast(I32), 0)
+        w_words = consts.tile([P, PASSES, 2 * D], U8, align_bytes=64)
+
+        def load_heads(i):
+            tok = slice(i * P, (i + 1) * P)
+            v_tile = per_tile.tile([P, KV_HEADS, HD], BF16)
+            nc.sync.dma_start(out=v_tile[:], in_=v_rows[tok])
+            a_tile = per_tile.tile([P, HEADS, HD], BF16)
+            nc.sync.dma_start(out=a_tile[:], in_=a_rows[tok])
+            v_tiles.append(v_tile)
+            a_tiles.append(a_tile)
+
+        def load_weight():
+            for q in range(4):
+                nc.sync.dma_start(
+                    out=w_planes[32 * q : 32 * q + 4, :, :].bitcast(I32),
+                    in_=wo_scales.bitcast(I32)[:, 4 * q : 4 * q + 4, :].rearrange("g r n -> r g n"),
+                )
+            nc.sync.dma_start(
+                out=w_words[:].bitcast(I32), in_=wo_words.bitcast(I32).rearrange("g p w -> p g w")
+            )
+
+        def load_residual(i):
+            x_tile = per_tile.tile([P, D], BF16)
+            nc.sync.dma_start(out=x_tile[:], in_=x_rows[i * P : (i + 1) * P, :])
+            x_tiles.append(x_tile)
+
+        nc.sync.dma_start(out=gain_rows[0:N_TILES, :], in_=attn_scale.rearrange("(r c) -> r c", c=P))
+        load_heads(0)
+        load_heads(1)
+        load_heads(2)
+        load_weight()
+        load_heads(3)
+        load_heads(4)
+        for i in range(TILES):
+            load_residual(i)
+
+        gain_rows_f32 = consts.tile([P, P], F32)
+        nc.scalar.copy(out=gain_rows_f32[:], in_=gain_rows[:])
+        turned = turn_psum.tile([P, PACK, P], F32)
+        nc.tensor.transpose(out=turned[:, 0, :], in_=gain_rows_f32[:], identity=ident[:])
+        gain = consts.tile([P, N_TILES], F32)
+        nc.scalar.copy(out=gain[:], in_=turned[:, 0, 0:N_TILES])
+
+        def norms(i):
+            squares = per_tile.tile([P, KV_HEADS, HD], BF16)
+            sumsq = per_tile.tile([P, KV_HEADS], F32)
+            for h in range(KV_HEADS):
+                nc.scalar.activation(
+                    out=squares[:, h, :],
+                    in_=v_tiles[i][:, h, :],
+                    func=ACT.Square,
+                    accum_out=sumsq[:, h : h + 1],
+                )
+            sumsq_tiles.append(sumsq)
+
+        def measure(i):
+            products = per_tile.tile([P, HEADS, HD], F32)
+            dots = per_tile.tile([P, HEADS], F32)
+            for hg in range(HEADS):
+                nc.vector.scalar_tensor_tensor(
+                    out=products[:, hg, :],
+                    in0=a_tiles[i][:, hg, :],
+                    scalar=1.0,
+                    in1=v_tiles[i][:, hg // GROUP, :],
+                    op0=ALU.mult,
+                    op1=ALU.mult,
+                    accum_out=dots[:, hg : hg + 1],
+                )
+            dot_tiles.append(dots)
+
+        def coefficients(i):
+            clamped = per_tile.tile([P, KV_HEADS], F32)
+            nc.vector.tensor_scalar_max(out=clamped[:], in0=sumsq_tiles[i][:], scalar1=MIN_NORM * MIN_NORM)
+            inverse = per_tile.tile([P, KV_HEADS], F32)
+            nc.vector.reciprocal(out=inverse[:], in_=clamped[:])
+            neg_coef = per_tile.tile([P, KV_HEADS, GROUP], F32)
+            nc.vector.scalar_tensor_tensor(
+                out=neg_coef[:],
+                in0=dot_tiles[i][:].rearrange("p (h g) -> p h g", g=GROUP),
+                scalar=-1.0,
+                in1=inverse[:].unsqueeze(2).to_broadcast([P, KV_HEADS, GROUP]),
+                op0=ALU.mult,
+                op1=ALU.mult,
+            )
+            coef_tiles.append(neg_coef)
+
+        def project(i):
+            y = per_tile.tile([P, C], BF16)
+            for hg in range(HEADS):
+                h, g = hg // GROUP, hg % GROUP
+                nc.vector.scalar_tensor_tensor(
+                    out=y[:, hg * HD : (hg + 1) * HD],
+                    in0=v_tiles[i][:, h, :],
+                    scalar=coef_tiles[i][:, h, g : g + 1],
+                    in1=a_tiles[i][:, hg, :],
+                    op0=ALU.mult,
+                    op1=ALU.add,
+                )
+            y_tiles.append(y)
+
+        def turn(i):
+            y_words = y_tiles[i][:].bitcast(F32)
+            words_per_pass = K_PASS // 2
+            turned = turn_psum.tile([P, PACK, P], F32)
+            for c in range(PASSES):
+                for u in range(2):
+                    nc.tensor.transpose(
+                        out=turned[:, 2 * c + u, :],
+                        in_=y_words[:, words_per_pass * c + u : words_per_pass * (c + 1) : 2],
+                        identity=ident[:],
+                    )
+            grouped = per_tile.tile([P, C], BF16, align_bytes=64)
+            nc.scalar.copy(
+                out=grouped[:].bitcast(F32).rearrange("p (c t u) -> p c t u", c=PASSES, u=2),
+                in_=turned[:].rearrange("p (c u) t -> p c t u", u=2),
+            )
+            grouped_tiles.append(grouped)
+
+        def quantise(i):
+            codes = per_tile.tile([P, PASSES * P], U32, align_bytes=64)
+            planes = per_tile.tile([P, PASSES * P], U8, align_bytes=64)
+            nc.vector.quantize_mx(out=codes[:].bitcast(FP8X4), scales=planes[:], in_=grouped_tiles[i][:])
+            code_tiles.append(codes)
+            plane_tiles.append(planes)
+
+        def multiply(i):
+            scaled = per_tile.tile([P, N_TILES, P], F32)
+            for half in range(HALVES):
+                acc = acc_psum.tile([P, BANK // P, P], F32)
+                for j in range(BANK // P):
+                    n = half * (BANK // P) + j
+                    for c in range(PASSES):
+                        nc.tensor.matmul_mx(
+                            out=acc[:, j, :],
+                            lhsT=w_words[:, c, 2 * P * n : 2 * P * (n + 1)].bitcast(FP4X4),
+                            lhsT_scale=w_planes[:, c, P * n : P * (n + 1)],
+                            rhs=code_tiles[i][:, P * c : P * (c + 1)].bitcast(FP8X4),
+                            rhs_scale=plane_tiles[i][:, P * c : P * (c + 1)],
+                            start=(c == 0),
+                            stop=(c == PASSES - 1),
+                        )
+                for j in range(BANK // P):
+                    n = half * (BANK // P) + j
+                    nc.scalar.activation(
+                        out=scaled[:, n, :], in_=acc[:, j, :], func=ACT.Copy, scale=gain[:, n : n + 1]
+                    )
+            scaled_tiles.append(scaled)
+
+        def turn_back(i):
+            halves = []
+            for half in range(HALVES):
+                back = back_psum.tile([P, BANK], F32)
+                for j in range(BANK // P):
+                    nc.tensor.transpose(
+                        out=back[:, j * P : (j + 1) * P],
+                        in_=scaled_tiles[i][:, half * (BANK // P) + j, :],
+                        identity=ident[:],
+                    )
+                halves.append(back)
+            back_tiles.append(halves)
+
+        def add_residual(i):
+            result = per_tile.tile([P, D], F32)
+            for half in range(HALVES):
+                cols = slice(half * BANK, (half + 1) * BANK)
+                nc.vector.tensor_tensor(
+                    out=result[:, cols], in0=back_tiles[i][half][:], in1=x_tiles[i][:, cols], op=ALU.add
+                )
+                nc.sync.dma_start(out=out_rows[i * P : (i + 1) * P, cols], in_=result[:, cols])
+
+        def live(i):
+            return 0 <= i < TILES
+
+        for s in range(-1, TILES + 4):
+            if live(s + 1):
+                norms(s + 1)
+            if live(s):
+                coefficients(s)
+            if live(s + 1):
+                measure(s + 1)
+            if live(s):
+                project(s)
+            if live(s - 1):
+                turn(s - 1)
+                quantise(s - 1)
+            if live(s - 2):
+                multiply(s - 2)
+            if live(s - 3):
+                turn_back(s - 3)
+            if live(s - 4):
+                add_residual(s - 4)

@@ -25,10 +25,12 @@ D = 1024
 PACK = 4
 K_PASS = P * PACK
 PASSES = C // K_PASS
-N_TILES = D // P
+HEADS_PER_PASS = K_PASS // HD
 BANK = 512
 HALVES = D // BANK
+BLOCKS = BANK // P
 MIN_NORM = 1e-12
+PARKED = 2
 
 FLOPS = 2 * TOKENS * C * D
 
@@ -44,12 +46,12 @@ def tile_block_pb_kernel(tc, attn_out, v, x, wo_words, wo_scales, attn_scale, ou
         consts = ctx.enter_context(tc.tile_pool(name="consts", bufs=1))
         per_tile = ctx.enter_context(tc.tile_pool(name="per_tile", bufs=TILES))
         turn_psum = ctx.enter_context(tc.psum_pool(name="turn_psum", bufs=2))
-        acc_psum = ctx.enter_context(tc.psum_pool(name="acc_psum", bufs=2))
-        back_psum = ctx.enter_context(tc.psum_pool(name="back_psum", bufs=4))
+        acc_psum = ctx.enter_context(tc.psum_pool(name="acc_psum", bufs=HALVES))
+        back_psum = ctx.enter_context(tc.psum_pool(name="back_psum", bufs=PARKED * HALVES))
         ctx.enter_context(tc.manual_schedule())
 
         a_tiles, v_tiles, x_tiles = [], [], []
-        sumsq_tiles, dot_tiles, coef_tiles = [], [], []
+        sumsq_tiles, clamped_tiles, neg_inverse_tiles, neg_coef_tiles = [], [], [], []
         y_tiles, grouped_tiles, code_tiles, plane_tiles = [], [], [], []
         scaled_tiles, back_tiles = [], []
 
@@ -60,14 +62,21 @@ def tile_block_pb_kernel(tc, attn_out, v, x, wo_words, wo_scales, attn_scale, ou
         w_planes = consts.tile([P, PASSES, D], U8, align_bytes=64)
         nc.vector.memset(w_planes[:].bitcast(I32), 0)
         w_words = consts.tile([P, PASSES, 2 * D], U8, align_bytes=64)
+        seed = consts.tile([P, 1], F32)
+        nc.vector.memset(seed[:], 0.0)
+        seed_squared = consts.tile([P, 1], F32)
+        nc.scalar.activation(out=seed_squared[:], in_=seed[:], func=ACT.Square)
+
+        def load_values(i):
+            v_tile = per_tile.tile([P, KV_HEADS, HD], BF16)
+            nc.sync.dma_start(out=v_tile[:], in_=v_rows[i * P : (i + 1) * P])
+            v_tiles.append(v_tile)
 
         def load_heads(i):
-            tok = slice(i * P, (i + 1) * P)
-            v_tile = per_tile.tile([P, KV_HEADS, HD], BF16)
-            nc.sync.dma_start(out=v_tile[:], in_=v_rows[tok])
             a_tile = per_tile.tile([P, HEADS, HD], BF16)
-            nc.sync.dma_start(out=a_tile[:], in_=a_rows[tok])
-            v_tiles.append(v_tile)
+            for c in range(PASSES):
+                heads = slice(c * HEADS_PER_PASS, (c + 1) * HEADS_PER_PASS)
+                nc.sync.dma_start(out=a_tile[:, heads, :], in_=a_rows[i * P : (i + 1) * P, heads, :])
             a_tiles.append(a_tile)
 
         def load_weight():
@@ -85,22 +94,26 @@ def tile_block_pb_kernel(tc, attn_out, v, x, wo_words, wo_scales, attn_scale, ou
             nc.sync.dma_start(out=x_tile[:], in_=x_rows[i * P : (i + 1) * P, :])
             x_tiles.append(x_tile)
 
-        nc.sync.dma_start(out=gain_rows[0:N_TILES, :], in_=attn_scale.rearrange("(r c) -> r c", c=P))
+        load_values(0)
         load_heads(0)
+        nc.sync.dma_start(out=gain_rows[0 : D // P, :], in_=attn_scale.rearrange("(r c) -> r c", c=P))
+        for i in range(1, TILES):
+            load_values(i)
         load_heads(1)
-        load_heads(2)
         load_weight()
-        load_heads(3)
-        load_heads(4)
+        for i in range(2, TILES):
+            load_heads(i)
         for i in range(TILES):
             load_residual(i)
 
-        gain_rows_f32 = consts.tile([P, P], F32)
-        nc.scalar.copy(out=gain_rows_f32[:], in_=gain_rows[:])
-        turned = turn_psum.tile([P, PACK, P], F32)
-        nc.tensor.transpose(out=turned[:, 0, :], in_=gain_rows_f32[:], identity=ident[:])
-        gain = consts.tile([P, N_TILES], F32)
-        nc.scalar.copy(out=gain[:], in_=turned[:, 0, 0:N_TILES])
+        gain = consts.tile([P, D // P], F32)
+
+        def prepare_gain():
+            gain_rows_f32 = consts.tile([P, P], F32)
+            nc.scalar.copy(out=gain_rows_f32[:], in_=gain_rows[:])
+            turned = turn_psum.tile([P, PACK, P], F32)
+            nc.tensor.transpose(out=turned[:, 0, :], in_=gain_rows_f32[:], identity=ident[:])
+            nc.scalar.copy(out=gain[:], in_=turned[:, 0, 0 : D // P])
 
         def norms(i):
             squares = per_tile.tile([P, KV_HEADS, HD], BF16)
@@ -114,45 +127,46 @@ def tile_block_pb_kernel(tc, attn_out, v, x, wo_words, wo_scales, attn_scale, ou
                 )
             sumsq_tiles.append(sumsq)
 
+        def clamp_norms(i):
+            clamped = per_tile.tile([P, KV_HEADS], F32)
+            nc.vector.tensor_scalar(
+                out=clamped[:],
+                in0=sumsq_tiles[i][:],
+                scalar1=MIN_NORM * MIN_NORM,
+                scalar2=-1.0,
+                op0=ALU.max,
+                op1=ALU.mult,
+            )
+            clamped_tiles.append(clamped)
+
+        def invert_norms(i):
+            neg_inverse = per_tile.tile([P, KV_HEADS], F32)
+            nc.vector.reciprocal(out=neg_inverse[:], in_=clamped_tiles[i][:])
+            neg_inverse_tiles.append(neg_inverse)
+
         def measure(i):
             products = per_tile.tile([P, HEADS, HD], F32)
-            dots = per_tile.tile([P, HEADS], F32)
+            neg_coef = per_tile.tile([P, HEADS], F32)
             for hg in range(HEADS):
+                h = hg // GROUP
                 nc.vector.scalar_tensor_tensor(
                     out=products[:, hg, :],
                     in0=a_tiles[i][:, hg, :],
-                    scalar=1.0,
-                    in1=v_tiles[i][:, hg // GROUP, :],
+                    scalar=neg_inverse_tiles[i][:, h : h + 1],
+                    in1=v_tiles[i][:, h, :],
                     op0=ALU.mult,
                     op1=ALU.mult,
-                    accum_out=dots[:, hg : hg + 1],
+                    accum_out=neg_coef[:, hg : hg + 1],
                 )
-            dot_tiles.append(dots)
-
-        def coefficients(i):
-            clamped = per_tile.tile([P, KV_HEADS], F32)
-            nc.vector.tensor_scalar_max(out=clamped[:], in0=sumsq_tiles[i][:], scalar1=MIN_NORM * MIN_NORM)
-            inverse = per_tile.tile([P, KV_HEADS], F32)
-            nc.vector.reciprocal(out=inverse[:], in_=clamped[:])
-            neg_coef = per_tile.tile([P, KV_HEADS, GROUP], F32)
-            nc.vector.scalar_tensor_tensor(
-                out=neg_coef[:],
-                in0=dot_tiles[i][:].rearrange("p (h g) -> p h g", g=GROUP),
-                scalar=-1.0,
-                in1=inverse[:].unsqueeze(2).to_broadcast([P, KV_HEADS, GROUP]),
-                op0=ALU.mult,
-                op1=ALU.mult,
-            )
-            coef_tiles.append(neg_coef)
+            neg_coef_tiles.append(neg_coef)
 
         def project(i):
             y = per_tile.tile([P, C], BF16)
             for hg in range(HEADS):
-                h, g = hg // GROUP, hg % GROUP
                 nc.vector.scalar_tensor_tensor(
                     out=y[:, hg * HD : (hg + 1) * HD],
-                    in0=v_tiles[i][:, h, :],
-                    scalar=coef_tiles[i][:, h, g : g + 1],
+                    in0=v_tiles[i][:, hg // GROUP, :],
+                    scalar=neg_coef_tiles[i][:, hg : hg + 1],
                     in1=a_tiles[i][:, hg, :],
                     op0=ALU.mult,
                     op1=ALU.add,
@@ -183,38 +197,37 @@ def tile_block_pb_kernel(tc, attn_out, v, x, wo_words, wo_scales, attn_scale, ou
             nc.vector.quantize_mx(out=codes[:].bitcast(FP8X4), scales=planes[:], in_=grouped_tiles[i][:])
             code_tiles.append(codes)
             plane_tiles.append(planes)
-
-        def multiply(i):
-            scaled = per_tile.tile([P, N_TILES, P], F32)
-            for half in range(HALVES):
-                acc = acc_psum.tile([P, BANK // P, P], F32)
-                for j in range(BANK // P):
-                    n = half * (BANK // P) + j
-                    for c in range(PASSES):
-                        nc.tensor.matmul_mx(
-                            out=acc[:, j, :],
-                            lhsT=w_words[:, c, 2 * P * n : 2 * P * (n + 1)].bitcast(FP4X4),
-                            lhsT_scale=w_planes[:, c, P * n : P * (n + 1)],
-                            rhs=code_tiles[i][:, P * c : P * (c + 1)].bitcast(FP8X4),
-                            rhs_scale=plane_tiles[i][:, P * c : P * (c + 1)],
-                            start=(c == 0),
-                            stop=(c == PASSES - 1),
-                        )
-                for j in range(BANK // P):
-                    n = half * (BANK // P) + j
-                    nc.scalar.activation(
-                        out=scaled[:, n, :], in_=acc[:, j, :], func=ACT.Copy, scale=gain[:, n : n + 1]
-                    )
+            scaled = per_tile.tile([P, D // P, P], F32)
             scaled_tiles.append(scaled)
+
+        def multiply(i, half):
+            acc = acc_psum.tile([P, BLOCKS, P], F32)
+            for j in range(BLOCKS):
+                n = half * BLOCKS + j
+                for c in range(PASSES):
+                    nc.tensor.matmul_mx(
+                        out=acc[:, j, :],
+                        lhsT=w_words[:, c, 2 * P * n : 2 * P * (n + 1)].bitcast(FP4X4),
+                        lhsT_scale=w_planes[:, c, P * n : P * (n + 1)],
+                        rhs=code_tiles[i][:, P * c : P * (c + 1)].bitcast(FP8X4),
+                        rhs_scale=plane_tiles[i][:, P * c : P * (c + 1)],
+                        start=(c == 0),
+                        stop=(c == PASSES - 1),
+                    )
+            for j in range(BLOCKS):
+                n = half * BLOCKS + j
+                nc.scalar.activation(
+                    out=scaled_tiles[i][:, n, :], in_=acc[:, j, :], func=ACT.Copy, scale=gain[:, n : n + 1]
+                )
 
         def turn_back(i):
             halves = []
             for half in range(HALVES):
                 back = back_psum.tile([P, BANK], F32)
-                for j in range(BANK // P):
+                for j in range(BLOCKS):
                     nc.tensor.transpose(
                         out=back[:, j * P : (j + 1) * P],
-                        in_=scaled_tiles[i][:, half * (BANK // P) + j, :],
+                        in_=scaled_tiles[i][:, half * BLOCKS + j, :],
                         identity=ident[:],
                     )
                 halves.append(back)
@@ -229,24 +242,34 @@ def tile_block_pb_kernel(tc, attn_out, v, x, wo_words, wo_scales, attn_scale, ou
                 )
                 nc.sync.dma_start(out=out_rows[i * P : (i + 1) * P, cols], in_=result[:, cols])
 
-        def live(i):
-            return 0 <= i < TILES
-
-        for s in range(-1, TILES + 4):
-            if live(s + 1):
-                norms(s + 1)
-            if live(s):
-                coefficients(s)
-            if live(s + 1):
-                measure(s + 1)
-            if live(s):
-                project(s)
-            if live(s - 1):
-                turn(s - 1)
-                quantise(s - 1)
-            if live(s - 2):
-                multiply(s - 2)
-            if live(s - 3):
-                turn_back(s - 3)
-            if live(s - 4):
-                add_residual(s - 4)
+        last = TILES - 1
+        norms(0)
+        prepare_gain()
+        for i in range(1, TILES):
+            norms(i)
+        clamp_norms(0)
+        invert_norms(0)
+        for i in range(TILES):
+            if i < last:
+                clamp_norms(i + 1)
+            measure(i)
+            if i < last:
+                invert_norms(i + 1)
+            if i >= 1:
+                quantise(i - 1)
+                multiply(i - 1, 0)
+            project(i)
+            turn(i)
+            if i >= 1:
+                multiply(i - 1, 1)
+            if 0 <= i - 2 < PARKED:
+                turn_back(i - 2)
+        add_residual(0)
+        turn_back(PARKED)
+        quantise(last)
+        for half in range(HALVES):
+            multiply(last, half)
+        for i in range(1, TILES):
+            add_residual(i)
+            if i + PARKED < TILES:
+                turn_back(i + PARKED)

@@ -48,7 +48,6 @@ def tile_block_pb_kernel(tc, attn_out, v, x, wo_words, wo_scales, attn_scale, ou
         turn_psum = ctx.enter_context(tc.psum_pool(name="turn_psum", bufs=2))
         acc_psum = ctx.enter_context(tc.psum_pool(name="acc_psum", bufs=HALVES))
         back_psum = ctx.enter_context(tc.psum_pool(name="back_psum", bufs=PARKED * HALVES))
-        ctx.enter_context(tc.manual_schedule())
 
         a_tiles, v_tiles, x_tiles = [], [], []
         sumsq_tiles, clamped_tiles, neg_inverse_tiles, neg_coef_tiles = [], [], [], []

@@ -48,6 +48,7 @@ def tile_block_pb_kernel(tc, attn_out, v, x, wo_words, wo_scales, attn_scale, ou
         turn_psum = ctx.enter_context(tc.psum_pool(name="turn_psum", bufs=2))
         acc_psum = ctx.enter_context(tc.psum_pool(name="acc_psum", bufs=HALVES))
         back_psum = ctx.enter_context(tc.psum_pool(name="back_psum", bufs=PARKED * HALVES))
+        ctx.enter_context(tc.manual_schedule())
 
         a_tiles, v_tiles, x_tiles = [], [], []
         sumsq_tiles, clamped_tiles, neg_inverse_tiles, neg_coef_tiles = [], [], [], []
@@ -242,21 +243,20 @@ def tile_block_pb_kernel(tc, attn_out, v, x, wo_words, wo_scales, attn_scale, ou
                 nc.sync.dma_start(out=out_rows[i * P : (i + 1) * P, cols], in_=result[:, cols])
 
         last = TILES - 1
-        norms(0)
-        prepare_gain()
-        for i in range(1, TILES):
+        for i in range(TILES):
             norms(i)
+        prepare_gain()
         clamp_norms(0)
         invert_norms(0)
         for i in range(TILES):
-            if i < last:
-                clamp_norms(i + 1)
             measure(i)
             if i < last:
-                invert_norms(i + 1)
+                clamp_norms(i + 1)
             if i >= 1:
                 quantise(i - 1)
                 multiply(i - 1, 0)
+            if i < last:
+                invert_norms(i + 1)
             project(i)
             turn(i)
             if i >= 1:

@@ -53,7 +53,7 @@ def tile_block_pb_kernel(tc, attn_out, v, x, wo_words, wo_scales, attn_scale, ou
         a_tiles, v_tiles, x_tiles = [], [], []
         sumsq_tiles, clamped_tiles, neg_inverse_tiles, neg_coef_tiles = [], [], [], []
         y_tiles, grouped_tiles, code_tiles, plane_tiles = [], [], [], []
-        scaled_tiles, back_tiles = [], []
+        acc_tiles, scaled_tiles, back_tiles = [], [], []
 
         ident = consts.tile([P, P], F32)
         make_identity(nc, ident[:])
@@ -111,7 +111,7 @@ def tile_block_pb_kernel(tc, attn_out, v, x, wo_words, wo_scales, attn_scale, ou
         def prepare_gain():
             gain_rows_f32 = consts.tile([P, P], F32)
             nc.scalar.copy(out=gain_rows_f32[:], in_=gain_rows[:])
-            turned = turn_psum.tile([P, PACK, P], F32)
+            turned = turn_psum.tile([P, 2, P], F32)
             nc.tensor.transpose(out=turned[:, 0, :], in_=gain_rows_f32[:], identity=ident[:])
             nc.scalar.copy(out=gain[:], in_=turned[:, 0, 0 : D // P])
 
@@ -176,19 +176,17 @@ def tile_block_pb_kernel(tc, attn_out, v, x, wo_words, wo_scales, attn_scale, ou
         def turn(i):
             y_words = y_tiles[i][:].bitcast(F32)
             words_per_pass = K_PASS // 2
-            turned = turn_psum.tile([P, PACK, P], F32)
+            grouped = per_tile.tile([P, C], BF16, align_bytes=64)
+            grouped_words = grouped[:].bitcast(F32).rearrange("p (c t u) -> p c t u", c=PASSES, u=2)
             for c in range(PASSES):
+                turned = turn_psum.tile([P, 2, P], F32)
                 for u in range(2):
                     nc.tensor.transpose(
-                        out=turned[:, 2 * c + u, :],
+                        out=turned[:, u, :],
                         in_=y_words[:, words_per_pass * c + u : words_per_pass * (c + 1) : 2],
                         identity=ident[:],
                     )
-            grouped = per_tile.tile([P, C], BF16, align_bytes=64)
-            nc.scalar.copy(
-                out=grouped[:].bitcast(F32).rearrange("p (c t u) -> p c t u", c=PASSES, u=2),
-                in_=turned[:].rearrange("p (c u) t -> p c t u", u=2),
-            )
+                nc.scalar.copy(out=grouped_words[:, c, :, :], in_=turned[:].rearrange("p u t -> p t u"))
             grouped_tiles.append(grouped)
 
         def quantise(i):
@@ -197,8 +195,7 @@ def tile_block_pb_kernel(tc, attn_out, v, x, wo_words, wo_scales, attn_scale, ou
             nc.vector.quantize_mx(out=codes[:].bitcast(FP8X4), scales=planes[:], in_=grouped_tiles[i][:])
             code_tiles.append(codes)
             plane_tiles.append(planes)
-            scaled = per_tile.tile([P, D // P, P], F32)
-            scaled_tiles.append(scaled)
+            acc_tiles.append([])
 
         def multiply(i, half):
             acc = acc_psum.tile([P, BLOCKS, P], F32)
@@ -214,11 +211,18 @@ def tile_block_pb_kernel(tc, attn_out, v, x, wo_words, wo_scales, attn_scale, ou
                         start=(c == 0),
                         stop=(c == PASSES - 1),
                     )
-            for j in range(BLOCKS):
-                n = half * BLOCKS + j
+            acc_tiles[i].append(acc)
+
+        def apply_gain(i):
+            scaled = per_tile.tile([P, D // P, P], F32)
+            for n in range(D // P):
                 nc.scalar.activation(
-                    out=scaled_tiles[i][:, n, :], in_=acc[:, j, :], func=ACT.Copy, scale=gain[:, n : n + 1]
+                    out=scaled[:, n, :],
+                    in_=acc_tiles[i][n // BLOCKS][:, n % BLOCKS, :],
+                    func=ACT.Copy,
+                    scale=gain[:, n : n + 1],
                 )
+            scaled_tiles.append(scaled)
 
         def turn_back(i):
             halves = []
@@ -261,6 +265,7 @@ def tile_block_pb_kernel(tc, attn_out, v, x, wo_words, wo_scales, attn_scale, ou
             turn(i)
             if i >= 1:
                 multiply(i - 1, 1)
+                apply_gain(i - 1)
             if 0 <= i - 2 < PARKED:
                 turn_back(i - 2)
         add_residual(0)
@@ -268,6 +273,7 @@ def tile_block_pb_kernel(tc, attn_out, v, x, wo_words, wo_scales, attn_scale, ou
         quantise(last)
         for half in range(HALVES):
             multiply(last, half)
+        apply_gain(last)
         for i in range(1, TILES):
             add_residual(i)
             if i + PARKED < TILES:

@@ -30,35 +30,32 @@ BANK = 512
 HALVES = D // BANK
 BLOCKS = BANK // P
 MIN_NORM = 1e-12
-PARKED = 2
+CHANNELS_FIRST = 3
 
 FLOPS = 2 * TOKENS * C * D
 
 
 def tile_block_pb_kernel(tc, attn_out, v, x, wo_words, wo_scales, attn_scale, out):
     nc = tc.nc
-    a_rows = attn_out.rearrange("b h g t d -> t (b h g) d")
-    v_rows = v.rearrange("b h t d -> t (b h) d")
-    x_rows = x.rearrange("b t n -> (b t) n")
-    out_rows = out.rearrange("b t n -> (b t) n")
+    a_rows = attn_out.rearrange("b h g (p i) d -> p (b h g) i d", i=TILES)
+    v_rows = v.rearrange("b h (p i) d -> p (b h) i d", i=TILES)
+    x_rows = x.rearrange("b (p i) n -> p (b i) n", i=TILES)
+    out_rows = out.rearrange("b (p i) n -> p (b i) n", i=TILES)
 
     with ExitStack() as ctx:
         consts = ctx.enter_context(tc.tile_pool(name="consts", bufs=1))
         per_tile = ctx.enter_context(tc.tile_pool(name="per_tile", bufs=TILES))
         turn_psum = ctx.enter_context(tc.psum_pool(name="turn_psum", bufs=2))
-        acc_psum = ctx.enter_context(tc.psum_pool(name="acc_psum", bufs=HALVES))
-        back_psum = ctx.enter_context(tc.psum_pool(name="back_psum", bufs=PARKED * HALVES))
+        acc_psum = ctx.enter_context(tc.psum_pool(name="acc_psum", bufs=3))
+        back_psum = ctx.enter_context(tc.psum_pool(name="back_psum", bufs=3))
         ctx.enter_context(tc.manual_schedule())
-
-        a_tiles, v_tiles, x_tiles = [], [], []
-        sumsq_tiles, clamped_tiles, neg_inverse_tiles, neg_coef_tiles = [], [], [], []
-        y_tiles, grouped_tiles, code_tiles, plane_tiles = [], [], [], []
-        acc_tiles, scaled_tiles, back_tiles = [], [], []
 
         ident = consts.tile([P, P], F32)
         make_identity(nc, ident[:])
+        ident_bf16 = consts.tile([P, P], BF16)
+        nc.gpsimd.tensor_copy(out=ident_bf16[:], in_=ident[:])
         gain_rows = consts.tile([P, P], BF16)
-        nc.gpsimd.memset(gain_rows[:], 0.0)
+        nc.vector.memset(gain_rows[:], 0.0)
         w_planes = consts.tile([P, PASSES, D], U8, align_bytes=64)
         nc.vector.memset(w_planes[:].bitcast(I32), 0)
         w_words = consts.tile([P, PASSES, 2 * D], U8, align_bytes=64)
@@ -67,71 +64,91 @@ def tile_block_pb_kernel(tc, attn_out, v, x, wo_words, wo_scales, attn_scale, ou
         seed_squared = consts.tile([P, 1], F32)
         nc.scalar.activation(out=seed_squared[:], in_=seed[:], func=ACT.Square)
 
-        def load_values(i):
-            v_tile = per_tile.tile([P, KV_HEADS, HD], BF16)
-            nc.sync.dma_start(out=v_tile[:], in_=v_rows[i * P : (i + 1) * P])
-            v_tiles.append(v_tile)
+        v_first = consts.tile([P, KV_HEADS, 1, HD], BF16)
+        a_first = consts.tile([P, HEADS, 1, HD], BF16)
+        v_rest = consts.tile([P, KV_HEADS, TILES - 1, HD], BF16)
+        a_pairs = [
+            [consts.tile([P, HEADS_PER_PASS, 2, HD], BF16, name="a_%d_%d" % (pair, c)) for c in range(PASSES)]
+            for pair in range(2)
+        ]
+        x_tiles = [consts.tile([P, D], BF16, name="x_%d" % i) for i in range(TILES)]
 
-        def load_heads(i):
-            a_tile = per_tile.tile([P, HEADS, HD], BF16)
-            for c in range(PASSES):
-                heads = slice(c * HEADS_PER_PASS, (c + 1) * HEADS_PER_PASS)
-                nc.sync.dma_start(out=a_tile[:, heads, :], in_=a_rows[i * P : (i + 1) * P, heads, :])
-            a_tiles.append(a_tile)
-
-        def load_weight():
-            for q in range(4):
-                nc.sync.dma_start(
-                    out=w_planes[32 * q : 32 * q + 4, :, :].bitcast(I32),
-                    in_=wo_scales.bitcast(I32)[:, 4 * q : 4 * q + 4, :].rearrange("g r n -> r g n"),
-                )
-            nc.sync.dma_start(
-                out=w_words[:].bitcast(I32), in_=wo_words.bitcast(I32).rearrange("g p w -> p g w")
-            )
-
-        def load_residual(i):
-            x_tile = per_tile.tile([P, D], BF16)
-            nc.sync.dma_start(out=x_tile[:], in_=x_rows[i * P : (i + 1) * P, :])
-            x_tiles.append(x_tile)
-
-        load_values(0)
-        load_heads(0)
         nc.sync.dma_start(out=gain_rows[0 : D // P, :], in_=attn_scale.rearrange("(r c) -> r c", c=P))
-        for i in range(1, TILES):
-            load_values(i)
-        load_heads(1)
-        load_weight()
-        for i in range(2, TILES):
-            load_heads(i)
+        for h in range(KV_HEADS):
+            heads = slice(h * GROUP, (h + 1) * GROUP)
+            nc.sync.dma_start(out=v_first[:, h, :, :], in_=v_rows[:, h, 0:1, :])
+            nc.sync.dma_start(out=a_first[:, heads, :, :], in_=a_rows[:, heads, 0:1, :])
+
+        def load_pair(pair):
+            for c in range(PASSES):
+                nc.sync.dma_start(
+                    out=a_pairs[pair][c][:],
+                    in_=a_rows[:, c * HEADS_PER_PASS : (c + 1) * HEADS_PER_PASS, 1 + 2 * pair : 3 + 2 * pair, :],
+                )
+
+        nc.sync.dma_start(out=v_rest[:], in_=v_rows[:, :, 1:TILES, :])
+        load_pair(0)
+        for q in range(4):
+            nc.sync.dma_start(
+                out=w_planes[32 * q : 32 * q + 4, :, :].bitcast(I32),
+                in_=wo_scales.bitcast(I32)[:, 4 * q : 4 * q + 4, :].rearrange("g r n -> r g n"),
+            )
+        nc.sync.dma_start(out=w_words[:].bitcast(I32), in_=wo_words.bitcast(I32).rearrange("g p w -> p g w"))
+        load_pair(1)
         for i in range(TILES):
-            load_residual(i)
+            nc.sync.dma_start(out=x_tiles[i][:], in_=x_rows[:, i, :])
+
+        def v_head(i, h):
+            return v_first[:, h, 0, :] if i == 0 else v_rest[:, h, i - 1, :]
+
+        def a_head(i, hg):
+            if i == 0:
+                return a_first[:, hg, 0, :]
+            return a_pairs[(i - 1) // 2][hg // HEADS_PER_PASS][:, hg % HEADS_PER_PASS, (i - 1) % 2, :]
 
         gain = consts.tile([P, D // P], F32)
+        gain_wide = consts.tile([P, D], F32)
+        gain_turned, gain_banks = [], []
 
         def prepare_gain():
             gain_rows_f32 = consts.tile([P, P], F32)
             nc.scalar.copy(out=gain_rows_f32[:], in_=gain_rows[:])
             turned = turn_psum.tile([P, 2, P], F32)
             nc.tensor.transpose(out=turned[:, 0, :], in_=gain_rows_f32[:], identity=ident[:])
-            nc.scalar.copy(out=gain[:], in_=turned[:, 0, 0 : D // P])
+            gain_turned.append(turned)
+
+        def spread_gain():
+            nc.scalar.copy(out=gain[:], in_=gain_turned[0][:, 0, 0 : D // P])
+            for half in range(HALVES):
+                back = back_psum.tile([P, BANK], F32)
+                for j in range(BLOCKS):
+                    n = half * BLOCKS + j
+                    nc.tensor.transpose(
+                        out=back[:, j * P : (j + 1) * P],
+                        in_=gain[:, n : n + 1].to_broadcast([P, P]),
+                        identity=ident[:],
+                    )
+                gain_banks.append(back)
+
+        def keep_gain():
+            for half in range(HALVES):
+                nc.scalar.copy(out=gain_wide[:, half * BANK : (half + 1) * BANK], in_=gain_banks[half][:])
+
+        sumsq_tiles, clamped_tiles, neg_inverse_tiles, neg_coef_tiles = [], [], [], []
+        y_tiles, code_tiles, plane_tiles, grouped_tiles = [], [], [], []
+        acc_tiles, scaled_tiles, back_tiles = {}, {}, {}
 
         def norms(i):
-            squares = per_tile.tile([P, KV_HEADS, HD], BF16)
+            squares = per_tile.tile([P, KV_HEADS, HD], F32)
             sumsq = per_tile.tile([P, KV_HEADS], F32)
             for h in range(KV_HEADS):
                 nc.scalar.activation(
-                    out=squares[:, h, :],
-                    in_=v_tiles[i][:, h, :],
-                    func=ACT.Square,
-                    accum_out=sumsq[:, h : h + 1],
+                    out=squares[:, h, :], in_=v_head(i, h), func=ACT.Square, accum_out=sumsq[:, h : h + 1]
                 )
-            sumsq_tiles.append(sumsq)
-
-        def clamp_norms(i):
             clamped = per_tile.tile([P, KV_HEADS], F32)
-            nc.vector.tensor_scalar(
+            nc.gpsimd.tensor_scalar(
                 out=clamped[:],
-                in0=sumsq_tiles[i][:],
+                in0=sumsq[:],
                 scalar1=MIN_NORM * MIN_NORM,
                 scalar2=-1.0,
                 op0=ALU.max,
@@ -144,20 +161,22 @@ def tile_block_pb_kernel(tc, attn_out, v, x, wo_words, wo_scales, attn_scale, ou
             nc.vector.reciprocal(out=neg_inverse[:], in_=clamped_tiles[i][:])
             neg_inverse_tiles.append(neg_inverse)
 
-        def measure(i):
+        def measure(i, scalar_of, sums, heads):
             products = per_tile.tile([P, HEADS, HD], F32)
-            neg_coef = per_tile.tile([P, HEADS], F32)
-            for hg in range(HEADS):
-                h = hg // GROUP
+            for hg in heads:
                 nc.vector.scalar_tensor_tensor(
                     out=products[:, hg, :],
-                    in0=a_tiles[i][:, hg, :],
-                    scalar=neg_inverse_tiles[i][:, h : h + 1],
-                    in1=v_tiles[i][:, h, :],
+                    in0=a_head(i, hg),
+                    scalar=scalar_of(hg // GROUP),
+                    in1=v_head(i, hg // GROUP),
                     op0=ALU.mult,
                     op1=ALU.mult,
-                    accum_out=neg_coef[:, hg : hg + 1],
+                    accum_out=sums[:, hg : hg + 1],
                 )
+
+        def measure_tile(i):
+            neg_coef = per_tile.tile([P, HEADS], F32)
+            measure(i, lambda h: neg_inverse_tiles[i][:, h : h + 1], neg_coef, range(HEADS))
             neg_coef_tiles.append(neg_coef)
 
         def project(i):
@@ -165,9 +184,9 @@ def tile_block_pb_kernel(tc, attn_out, v, x, wo_words, wo_scales, attn_scale, ou
             for hg in range(HEADS):
                 nc.vector.scalar_tensor_tensor(
                     out=y[:, hg * HD : (hg + 1) * HD],
-                    in0=v_tiles[i][:, hg // GROUP, :],
+                    in0=v_head(i, hg // GROUP),
                     scalar=neg_coef_tiles[i][:, hg : hg + 1],
-                    in1=a_tiles[i][:, hg, :],
+                    in1=a_head(i, hg),
                     op0=ALU.mult,
                     op1=ALU.add,
                 )
@@ -176,8 +195,7 @@ def tile_block_pb_kernel(tc, attn_out, v, x, wo_words, wo_scales, attn_scale, ou
         def turn(i):
             y_words = y_tiles[i][:].bitcast(F32)
             words_per_pass = K_PASS // 2
-            grouped = per_tile.tile([P, C], BF16, align_bytes=64)
-            grouped_words = grouped[:].bitcast(F32).rearrange("p (c t u) -> p c t u", c=PASSES, u=2)
+            turned_tiles = []
             for c in range(PASSES):
                 turned = turn_psum.tile([P, 2, P], F32)
                 for u in range(2):
@@ -186,95 +204,172 @@ def tile_block_pb_kernel(tc, attn_out, v, x, wo_words, wo_scales, attn_scale, ou
                         in_=y_words[:, words_per_pass * c + u : words_per_pass * (c + 1) : 2],
                         identity=ident[:],
                     )
-                nc.scalar.copy(out=grouped_words[:, c, :, :], in_=turned[:].rearrange("p u t -> p t u"))
+                turned_tiles.append(turned)
+            grouped = per_tile.tile([P, C], BF16, align_bytes=64)
+            grouped_words = grouped[:].bitcast(F32).rearrange("p (c t u) -> p c t u", c=PASSES, u=2)
+            for c in range(PASSES):
+                nc.scalar.copy(out=grouped_words[:, c, :, :], in_=turned_tiles[c][:].rearrange("p u t -> p t u"))
             grouped_tiles.append(grouped)
 
-        def quantise(i):
+        def quantise_columns(i, cols):
+            nc.vector.quantize_mx(
+                out=code_tiles[i][:, cols].bitcast(FP8X4),
+                scales=plane_tiles[i][:, cols],
+                in_=grouped_tiles[i][:, PACK * cols.start : PACK * cols.stop],
+            )
+
+        def open_codes(i):
             codes = per_tile.tile([P, PASSES * P], U32, align_bytes=64)
             planes = per_tile.tile([P, PASSES * P], U8, align_bytes=64)
-            nc.vector.quantize_mx(out=codes[:].bitcast(FP8X4), scales=planes[:], in_=grouped_tiles[i][:])
             code_tiles.append(codes)
             plane_tiles.append(planes)
-            acc_tiles.append([])
 
-        def multiply(i, half):
-            acc = acc_psum.tile([P, BLOCKS, P], F32)
-            for j in range(BLOCKS):
-                n = half * BLOCKS + j
-                for c in range(PASSES):
-                    nc.tensor.matmul_mx(
-                        out=acc[:, j, :],
-                        lhsT=w_words[:, c, 2 * P * n : 2 * P * (n + 1)].bitcast(FP4X4),
-                        lhsT_scale=w_planes[:, c, P * n : P * (n + 1)],
-                        rhs=code_tiles[i][:, P * c : P * (c + 1)].bitcast(FP8X4),
-                        rhs_scale=plane_tiles[i][:, P * c : P * (c + 1)],
-                        start=(c == 0),
-                        stop=(c == PASSES - 1),
-                    )
-            acc_tiles[i].append(acc)
+        def quantise(i):
+            open_codes(i)
+            quantise_columns(i, slice(0, PASSES * P))
+
+        def multiply_channels(i):
+            for half in range(HALVES):
+                acc = acc_psum.tile([P, BLOCKS, P], F32)
+                for j in range(BLOCKS):
+                    n = half * BLOCKS + j
+                    for c in range(PASSES):
+                        nc.tensor.matmul_mx(
+                            out=acc[:, j, :],
+                            lhsT=w_words[:, c, 2 * P * n : 2 * P * (n + 1)].bitcast(FP4X4),
+                            lhsT_scale=w_planes[:, c, P * n : P * (n + 1)],
+                            rhs=code_tiles[i][:, P * c : P * (c + 1)].bitcast(FP8X4),
+                            rhs_scale=plane_tiles[i][:, P * c : P * (c + 1)],
+                            start=(c == 0),
+                            stop=(c == PASSES - 1),
+                        )
+                acc_tiles[i, half] = acc
 
         def apply_gain(i):
             scaled = per_tile.tile([P, D // P, P], F32)
             for n in range(D // P):
                 nc.scalar.activation(
                     out=scaled[:, n, :],
-                    in_=acc_tiles[i][n // BLOCKS][:, n % BLOCKS, :],
+                    in_=acc_tiles[i, n // BLOCKS][:, n % BLOCKS, :],
                     func=ACT.Copy,
                     scale=gain[:, n : n + 1],
                 )
-            scaled_tiles.append(scaled)
+            scaled_tiles[i] = scaled
 
         def turn_back(i):
-            halves = []
             for half in range(HALVES):
                 back = back_psum.tile([P, BANK], F32)
-                for j in range(BLOCKS):
-                    nc.tensor.transpose(
-                        out=back[:, j * P : (j + 1) * P],
-                        in_=scaled_tiles[i][:, half * BLOCKS + j, :],
-                        identity=ident[:],
-                    )
-                halves.append(back)
-            back_tiles.append(halves)
-
-        def add_residual(i):
-            result = per_tile.tile([P, D], F32)
-            for half in range(HALVES):
-                cols = slice(half * BANK, (half + 1) * BANK)
-                nc.vector.tensor_tensor(
-                    out=result[:, cols], in0=back_tiles[i][half][:], in1=x_tiles[i][:, cols], op=ALU.add
+                nc.tensor.matmul(
+                    out=back[:],
+                    lhsT=ident_bf16[:],
+                    rhs=x_tiles[i][:, half * BANK : (half + 1) * BANK],
+                    start=True,
+                    stop=False,
                 )
-                nc.sync.dma_start(out=out_rows[i * P : (i + 1) * P, cols], in_=result[:, cols])
+                for j in range(BLOCKS):
+                    nc.tensor.matmul(
+                        out=back[:, j * P : (j + 1) * P],
+                        lhsT=scaled_tiles[i][:, half * BLOCKS + j, :],
+                        rhs=ident[:],
+                        is_transpose=True,
+                        start=False,
+                        stop=(j == BLOCKS - 1),
+                    )
+                back_tiles[i, half] = back
+
+        def store(i, half, result):
+            nc.sync.dma_start(out=out_rows[:, i, half * BANK : (half + 1) * BANK], in_=result[:])
+
+        def copy_out(i, half):
+            result = per_tile.tile([P, BANK], F32, name="result_%d" % half)
+            nc.scalar.copy(out=result[:], in_=back_tiles[i, half][:])
+            store(i, half, result)
+
+        def multiply_tokens(i):
+            for half in range(HALVES):
+                acc = acc_psum.tile([P, BLOCKS, P], F32)
+                flat = acc[:].rearrange("p j t -> p (j t)")
+                for c in range(PASSES):
+                    nc.tensor.matmul_mx(
+                        out=flat,
+                        lhsT=code_tiles[i][:, P * c : P * (c + 1)].bitcast(FP8X4),
+                        lhsT_scale=plane_tiles[i][:, P * c : P * (c + 1)],
+                        rhs=w_words[:, c, 2 * BANK * half : 2 * BANK * (half + 1)].bitcast(FP4X4),
+                        rhs_scale=w_planes[:, c, BANK * half : BANK * (half + 1)],
+                        start=(c == 0),
+                        stop=(c == PASSES - 1),
+                    )
+                acc_tiles[i, half] = flat
+
+        def widen_gain(i, half):
+            product = per_tile.tile([P, BANK], F32, name="product_%d" % half)
+            nc.vector.tensor_tensor(
+                out=product[:],
+                in0=acc_tiles[i, half],
+                in1=gain_wide[:, half * BANK : (half + 1) * BANK],
+                op=ALU.mult,
+            )
+            scaled_tiles[i, half] = product
+
+        def add_residual(i, half):
+            result = per_tile.tile([P, BANK], F32, name="result_%d" % half)
+            nc.vector.tensor_tensor(
+                out=result[:],
+                in0=scaled_tiles[i, half][:],
+                in1=x_tiles[i][:, half * BANK : (half + 1) * BANK],
+                op=ALU.add,
+            )
+            store(i, half, result)
 
         last = TILES - 1
-        for i in range(TILES):
-            norms(i)
         prepare_gain()
-        clamp_norms(0)
+        norms(0)
+        spread_gain()
+        dots = consts.tile([P, HEADS], F32)
+        measure(0, lambda h: 1.0, dots, range(HEADS))
         invert_norms(0)
-        for i in range(TILES):
-            measure(i)
-            if i < last:
-                clamp_norms(i + 1)
-            if i >= 1:
-                quantise(i - 1)
-                multiply(i - 1, 0)
+        first_coef = per_tile.tile([P, HEADS], F32, name="neg_coef")
+        nc.vector.tensor_tensor(
+            out=first_coef[:].rearrange("p (h g) -> p h g", g=GROUP),
+            in0=dots[:].rearrange("p (h g) -> p h g", g=GROUP),
+            in1=neg_inverse_tiles[0][:].unsqueeze(2).to_broadcast([P, KV_HEADS, GROUP]),
+            op=ALU.mult,
+        )
+        neg_coef_tiles.append(first_coef)
+        norms(1)
+        norms(2)
+        project(0)
+        turn(0)
+        norms(3)
+        norms(4)
+        keep_gain()
+        for i in range(1, TILES):
+            if i == 1:
+                invert_norms(1)
+            measure_tile(i)
             if i < last:
                 invert_norms(i + 1)
+            quantise(i - 1)
             project(i)
+            if i - 1 < CHANNELS_FIRST:
+                multiply_channels(i - 1)
+            else:
+                multiply_tokens(i - 1)
             turn(i)
-            if i >= 1:
-                multiply(i - 1, 1)
+            if i - 1 < CHANNELS_FIRST:
                 apply_gain(i - 1)
-            if 0 <= i - 2 < PARKED:
+            if i >= 2:
                 turn_back(i - 2)
-        add_residual(0)
-        turn_back(PARKED)
-        quantise(last)
+                for half in range(HALVES):
+                    copy_out(i - 2, half)
         for half in range(HALVES):
-            multiply(last, half)
-        apply_gain(last)
-        for i in range(1, TILES):
-            add_residual(i)
-            if i + PARKED < TILES:
-                turn_back(i + PARKED)
+            widen_gain(last - 1, half)
+        open_codes(last)
+        for c in range(PASSES):
+            quantise_columns(last, slice(P * c, P * (c + 1)))
+            add_residual(last - 1, c)
+        multiply_tokens(last)
+        for half in range(HALVES):
+            widen_gain(last, half)
+        for half in range(HALVES):
+            add_residual(last, half)

@@ -145,10 +145,13 @@ def tile_block_pb_kernel(tc, attn_out, v, x, wo_words, wo_scales, attn_scale, ou
                 nc.scalar.activation(
                     out=squares[:, h, :], in_=v_head(i, h), func=ACT.Square, accum_out=sumsq[:, h : h + 1]
                 )
+            sumsq_tiles.append(sumsq)
+
+        def clamp_norms(i):
             clamped = per_tile.tile([P, KV_HEADS], F32)
-            nc.gpsimd.tensor_scalar(
+            nc.vector.tensor_scalar(
                 out=clamped[:],
-                in0=sumsq[:],
+                in0=sumsq_tiles[i][:],
                 scalar1=MIN_NORM * MIN_NORM,
                 scalar2=-1.0,
                 op0=ALU.max,
@@ -326,7 +329,9 @@ def tile_block_pb_kernel(tc, attn_out, v, x, wo_words, wo_scales, attn_scale, ou
         norms(0)
         spread_gain()
         dots = consts.tile([P, HEADS], F32)
-        measure(0, lambda h: 1.0, dots, range(HEADS))
+        measure(0, lambda h: 1.0, dots, range(HEADS - GROUP))
+        clamp_norms(0)
+        measure(0, lambda h: 1.0, dots, range(HEADS - GROUP, HEADS))
         invert_norms(0)
         first_coef = per_tile.tile([P, HEADS], F32, name="neg_coef")
         nc.vector.tensor_tensor(
@@ -339,17 +344,19 @@ def tile_block_pb_kernel(tc, attn_out, v, x, wo_words, wo_scales, attn_scale, ou
         norms(1)
         norms(2)
         project(0)
+        clamp_norms(1)
+        invert_norms(1)
         turn(0)
         norms(3)
         norms(4)
         keep_gain()
         for i in range(1, TILES):
-            if i == 1:
-                invert_norms(1)
             measure_tile(i)
             if i < last:
-                invert_norms(i + 1)
+                clamp_norms(i + 1)
             quantise(i - 1)
+            if i < last:
+                invert_norms(i + 1)
             project(i)
             if i - 1 < CHANNELS_FIRST:
                 multiply_channels(i - 1)

@@ -73,11 +73,11 @@ def tile_block_pb_kernel(tc, attn_out, v, x, wo_words, wo_scales, attn_scale, ou
         ]
         x_tiles = [consts.tile([P, D], BF16, name="x_%d" % i) for i in range(TILES)]
 
-        nc.sync.dma_start(out=gain_rows[0 : D // P, :], in_=attn_scale.rearrange("(r c) -> r c", c=P))
-        for h in range(KV_HEADS):
-            heads = slice(h * GROUP, (h + 1) * GROUP)
-            nc.sync.dma_start(out=v_first[:, h, :, :], in_=v_rows[:, h, 0:1, :])
+        nc.sync.dma_start(out=v_first[:], in_=v_rows[:, :, 0:1, :])
+        for c in range(PASSES):
+            heads = slice(c * HEADS_PER_PASS, (c + 1) * HEADS_PER_PASS)
             nc.sync.dma_start(out=a_first[:, heads, :, :], in_=a_rows[:, heads, 0:1, :])
+        nc.sync.dma_start(out=gain_rows[0 : D // P, :], in_=attn_scale.rearrange("(r c) -> r c", c=P))
 
         def load_pair(pair):
             for c in range(PASSES):
@@ -325,8 +325,8 @@ def tile_block_pb_kernel(tc, attn_out, v, x, wo_words, wo_scales, attn_scale, ou
             store(i, half, result)
 
         last = TILES - 1
-        prepare_gain()
         norms(0)
+        prepare_gain()
         spread_gain()
         dots = consts.tile([P, HEADS], F32)
         measure(0, lambda h: 1.0, dots, range(HEADS - GROUP))

@@ -358,11 +358,11 @@ def tile_block_pb_kernel(tc, attn_out, v, x, wo_words, wo_scales, attn_scale, ou
             if i < last:
                 invert_norms(i + 1)
             project(i)
+            turn(i)
             if i - 1 < CHANNELS_FIRST:
                 multiply_channels(i - 1)
             else:
                 multiply_tokens(i - 1)
-            turn(i)
             if i - 1 < CHANNELS_FIRST:
                 apply_gain(i - 1)
             if i >= 2:

@@ -77,6 +77,11 @@ def tile_block_pb_kernel(tc, attn_out, v, x, wo_words, wo_scales, attn_scale, ou
         for c in range(PASSES):
             heads = slice(c * HEADS_PER_PASS, (c + 1) * HEADS_PER_PASS)
             nc.sync.dma_start(out=a_first[:, heads, :, :], in_=a_rows[:, heads, 0:1, :])
+        for q in range(4):
+            nc.sync.dma_start(
+                out=w_planes[32 * q : 32 * q + 4, :, :].bitcast(I32),
+                in_=wo_scales.bitcast(I32)[:, 4 * q : 4 * q + 4, :].rearrange("g r n -> r g n"),
+            )
         nc.sync.dma_start(out=gain_rows[0 : D // P, :], in_=attn_scale.rearrange("(r c) -> r c", c=P))
 
         def load_pair(pair):
@@ -88,11 +93,6 @@ def tile_block_pb_kernel(tc, attn_out, v, x, wo_words, wo_scales, attn_scale, ou
 
         nc.sync.dma_start(out=v_rest[:], in_=v_rows[:, :, 1:TILES, :])
         load_pair(0)
-        for q in range(4):
-            nc.sync.dma_start(
-                out=w_planes[32 * q : 32 * q + 4, :, :].bitcast(I32),
-                in_=wo_scales.bitcast(I32)[:, 4 * q : 4 * q + 4, :].rearrange("g r n -> r g n"),
-            )
         nc.sync.dma_start(out=w_words[:].bitcast(I32), in_=wo_words.bitcast(I32).rearrange("g p w -> p g w"))
         load_pair(1)
         for i in range(TILES):
@@ -358,11 +358,12 @@ def tile_block_pb_kernel(tc, attn_out, v, x, wo_words, wo_scales, attn_scale, ou
             if i < last:
                 invert_norms(i + 1)
             project(i)
-            turn(i)
-            if i - 1 < CHANNELS_FIRST:
+            if i < last:
+                turn(i)
                 multiply_channels(i - 1)
             else:
                 multiply_tokens(i - 1)
+                turn(i)
             if i - 1 < CHANNELS_FIRST:
                 apply_gain(i - 1)
             if i >= 2:

@@ -97,6 +97,8 @@ def tile_block_pb_kernel(tc, attn_out, v, x, wo_words, wo_scales, attn_scale, ou
         load_pair(1)
         for i in range(TILES):
             nc.sync.dma_start(out=x_tiles[i][:], in_=x_rows[:, i, :])
+        gain_wide = consts.tile([P, D], BF16)
+        nc.sync.dma_start(out=gain_wide[:], in_=attn_scale.partition_broadcast(P))
 
         def v_head(i, h):
             return v_first[:, h, 0, :] if i == 0 else v_rest[:, h, i - 1, :]
@@ -107,8 +109,7 @@ def tile_block_pb_kernel(tc, attn_out, v, x, wo_words, wo_scales, attn_scale, ou
             return a_pairs[(i - 1) // 2][hg // HEADS_PER_PASS][:, hg % HEADS_PER_PASS, (i - 1) % 2, :]
 
         gain = consts.tile([P, D // P], F32)
-        gain_wide = consts.tile([P, D], F32)
-        gain_turned, gain_banks = [], []
+        gain_turned = []
 
         def prepare_gain():
             gain_rows_f32 = consts.tile([P, P], F32)
@@ -117,22 +118,8 @@ def tile_block_pb_kernel(tc, attn_out, v, x, wo_words, wo_scales, attn_scale, ou
             nc.tensor.transpose(out=turned[:, 0, :], in_=gain_rows_f32[:], identity=ident[:])
             gain_turned.append(turned)
 
-        def spread_gain():
-            nc.scalar.copy(out=gain[:], in_=gain_turned[0][:, 0, 0 : D // P])
-            for half in range(HALVES):
-                back = back_psum.tile([P, BANK], F32)
-                for j in range(BLOCKS):
-                    n = half * BLOCKS + j
-                    nc.tensor.transpose(
-                        out=back[:, j * P : (j + 1) * P],
-                        in_=gain[:, n : n + 1].to_broadcast([P, P]),
-                        identity=ident[:],
-                    )
-                gain_banks.append(back)
-
         def keep_gain():
-            for half in range(HALVES):
-                nc.scalar.copy(out=gain_wide[:, half * BANK : (half + 1) * BANK], in_=gain_banks[half][:])
+            nc.scalar.copy(out=gain[:], in_=gain_turned[0][:, 0, 0 : D // P])
 
         sumsq_tiles, clamped_tiles, neg_inverse_tiles, neg_coef_tiles = [], [], [], []
         y_tiles, code_tiles, plane_tiles, grouped_tiles = [], [], [], []
@@ -326,8 +313,6 @@ def tile_block_pb_kernel(tc, attn_out, v, x, wo_words, wo_scales, attn_scale, ou
 
         last = TILES - 1
         norms(0)
-        prepare_gain()
-        spread_gain()
         dots = consts.tile([P, HEADS], F32)
         measure(0, lambda h: 1.0, dots, range(HEADS - GROUP))
         clamp_norms(0)
@@ -342,12 +327,13 @@ def tile_block_pb_kernel(tc, attn_out, v, x, wo_words, wo_scales, attn_scale, ou
         )
         neg_coef_tiles.append(first_coef)
         norms(1)
-        norms(2)
         project(0)
         clamp_norms(1)
         invert_norms(1)
+        norms(2)
         turn(0)
         norms(3)
+        prepare_gain()
         norms(4)
         keep_gain()
         for i in range(1, TILES):

@@ -30,6 +30,7 @@ BANK = 512
 HALVES = D // BANK
 BLOCKS = BANK // P
 MIN_NORM = 1e-12
+SINGLE_TILES = 3
 CHANNELS_FIRST = 3
 
 FLOPS = 2 * TOKENS * C * D
@@ -64,49 +65,51 @@ def tile_block_pb_kernel(tc, attn_out, v, x, wo_words, wo_scales, attn_scale, ou
         seed_squared = consts.tile([P, 1], F32)
         nc.scalar.activation(out=seed_squared[:], in_=seed[:], func=ACT.Square)
 
-        v_first = consts.tile([P, KV_HEADS, 1, HD], BF16)
-        a_first = consts.tile([P, HEADS, 1, HD], BF16)
-        v_rest = consts.tile([P, KV_HEADS, TILES - 1, HD], BF16)
-        a_pairs = [
-            [consts.tile([P, HEADS_PER_PASS, 2, HD], BF16, name="a_%d_%d" % (pair, c)) for c in range(PASSES)]
-            for pair in range(2)
+        groups = [slice(i, i + 1) for i in range(SINGLE_TILES)] + [slice(SINGLE_TILES, TILES)]
+        group_of = [g for g, tiles in enumerate(groups) for i in range(tiles.start, tiles.stop)]
+        v_loads = [
+            consts.tile([P, KV_HEADS, tiles.stop - tiles.start, HD], BF16, name="v_%d" % tiles.start)
+            for tiles in groups
+        ]
+        a_loads = [
+            consts.tile([P, HEADS, tiles.stop - tiles.start, HD], BF16, name="a_%d" % tiles.start)
+            for tiles in groups
         ]
         x_tiles = [consts.tile([P, D], BF16, name="x_%d" % i) for i in range(TILES)]
 
-        nc.sync.dma_start(out=v_first[:], in_=v_rows[:, :, 0:1, :])
-        for c in range(PASSES):
-            heads = slice(c * HEADS_PER_PASS, (c + 1) * HEADS_PER_PASS)
-            nc.sync.dma_start(out=a_first[:, heads, :, :], in_=a_rows[:, heads, 0:1, :])
+        def load_heads(g):
+            tiles = groups[g]
+            nc.sync.dma_start(out=v_loads[g][:], in_=v_rows[:, :, tiles, :])
+            for c in range(PASSES):
+                heads = slice(c * HEADS_PER_PASS, (c + 1) * HEADS_PER_PASS)
+                nc.sync.dma_start(out=a_loads[g][:, heads, :, :], in_=a_rows[:, heads, tiles, :])
+
+        def load_residual(i):
+            nc.sync.dma_start(out=x_tiles[i][:], in_=x_rows[:, i, :])
+
+        load_heads(0)
         for q in range(4):
             nc.sync.dma_start(
                 out=w_planes[32 * q : 32 * q + 4, :, :].bitcast(I32),
                 in_=wo_scales.bitcast(I32)[:, 4 * q : 4 * q + 4, :].rearrange("g r n -> r g n"),
             )
+        load_heads(1)
         nc.sync.dma_start(out=gain_rows[0 : D // P, :], in_=attn_scale.rearrange("(r c) -> r c", c=P))
-
-        def load_pair(pair):
-            for c in range(PASSES):
-                nc.sync.dma_start(
-                    out=a_pairs[pair][c][:],
-                    in_=a_rows[:, c * HEADS_PER_PASS : (c + 1) * HEADS_PER_PASS, 1 + 2 * pair : 3 + 2 * pair, :],
-                )
-
-        nc.sync.dma_start(out=v_rest[:], in_=v_rows[:, :, 1:TILES, :])
-        load_pair(0)
         nc.sync.dma_start(out=w_words[:].bitcast(I32), in_=wo_words.bitcast(I32).rearrange("g p w -> p g w"))
-        load_pair(1)
+        for g in range(2, len(groups)):
+            load_heads(g)
         for i in range(TILES):
-            nc.sync.dma_start(out=x_tiles[i][:], in_=x_rows[:, i, :])
+            load_residual(i)
         gain_wide = consts.tile([P, D], BF16)
         nc.sync.dma_start(out=gain_wide[:], in_=attn_scale.partition_broadcast(P))
 
         def v_head(i, h):
-            return v_first[:, h, 0, :] if i == 0 else v_rest[:, h, i - 1, :]
+            g = group_of[i]
+            return v_loads[g][:, h, i - groups[g].start, :]
 
         def a_head(i, hg):
-            if i == 0:
-                return a_first[:, hg, 0, :]
-            return a_pairs[(i - 1) // 2][hg // HEADS_PER_PASS][:, hg % HEADS_PER_PASS, (i - 1) % 2, :]
+            g = group_of[i]
+            return a_loads[g][:, hg, i - groups[g].start, :]
 
         gain = consts.tile([P, D // P], F32)
         gain_turned = []
@@ -169,9 +172,12 @@ def tile_block_pb_kernel(tc, attn_out, v, x, wo_words, wo_scales, attn_scale, ou
             measure(i, lambda h: neg_inverse_tiles[i][:, h : h + 1], neg_coef, range(HEADS))
             neg_coef_tiles.append(neg_coef)
 
-        def project(i):
-            y = per_tile.tile([P, C], BF16)
-            for hg in range(HEADS):
+        def project(i, heads):
+            if i == len(y_tiles):
+                y = per_tile.tile([P, C], BF16)
+                y_tiles.append(y)
+            y = y_tiles[i]
+            for hg in heads:
                 nc.vector.scalar_tensor_tensor(
                     out=y[:, hg * HD : (hg + 1) * HD],
                     in0=v_head(i, hg // GROUP),
@@ -180,7 +186,6 @@ def tile_block_pb_kernel(tc, attn_out, v, x, wo_words, wo_scales, attn_scale, ou
                     op0=ALU.mult,
                     op1=ALU.add,
                 )
-            y_tiles.append(y)
 
         def turn(i):
             y_words = y_tiles[i][:].bitcast(F32)
@@ -327,9 +332,11 @@ def tile_block_pb_kernel(tc, attn_out, v, x, wo_words, wo_scales, attn_scale, ou
         )
         neg_coef_tiles.append(first_coef)
         norms(1)
-        project(0)
+        project(0, range(HEADS_PER_PASS))
         clamp_norms(1)
+        project(0, range(HEADS_PER_PASS, HEADS - GROUP))
         invert_norms(1)
+        project(0, range(HEADS - GROUP, HEADS))
         norms(2)
         turn(0)
         norms(3)
@@ -343,7 +350,7 @@ def tile_block_pb_kernel(tc, attn_out, v, x, wo_words, wo_scales, attn_scale, ou
             quantise(i - 1)
             if i < last:
                 invert_norms(i + 1)
-            project(i)
+            project(i, range(HEADS))
             if i < last:
                 turn(i)
                 multiply_channels(i - 1)

@@ -77,27 +77,32 @@ def tile_block_pb_kernel(tc, attn_out, v, x, wo_words, wo_scales, attn_scale, ou
         ]
         x_tiles = [consts.tile([P, D], BF16, name="x_%d" % i) for i in range(TILES)]
 
+        def load_values(g):
+            nc.sync.dma_start(out=v_loads[g][:], in_=v_rows[:, :, groups[g], :])
+
         def load_heads(g):
-            tiles = groups[g]
-            nc.sync.dma_start(out=v_loads[g][:], in_=v_rows[:, :, tiles, :])
             for c in range(PASSES):
                 heads = slice(c * HEADS_PER_PASS, (c + 1) * HEADS_PER_PASS)
-                nc.sync.dma_start(out=a_loads[g][:, heads, :, :], in_=a_rows[:, heads, tiles, :])
+                nc.sync.dma_start(out=a_loads[g][:, heads, :, :], in_=a_rows[:, heads, groups[g], :])
 
         def load_residual(i):
             nc.sync.dma_start(out=x_tiles[i][:], in_=x_rows[:, i, :])
 
+        load_values(0)
         load_heads(0)
         for q in range(4):
             nc.sync.dma_start(
                 out=w_planes[32 * q : 32 * q + 4, :, :].bitcast(I32),
                 in_=wo_scales.bitcast(I32)[:, 4 * q : 4 * q + 4, :].rearrange("g r n -> r g n"),
             )
+        load_values(1)
         load_heads(1)
+        load_values(2)
         nc.sync.dma_start(out=gain_rows[0 : D // P, :], in_=attn_scale.rearrange("(r c) -> r c", c=P))
         nc.sync.dma_start(out=w_words[:].bitcast(I32), in_=wo_words.bitcast(I32).rearrange("g p w -> p g w"))
-        for g in range(2, len(groups)):
-            load_heads(g)
+        load_heads(2)
+        load_values(3)
+        load_heads(3)
         for i in range(TILES):
             load_residual(i)
         gain_wide = consts.tile([P, D], BF16)
@@ -337,11 +342,9 @@ def tile_block_pb_kernel(tc, attn_out, v, x, wo_words, wo_scales, attn_scale, ou
         project(0, range(HEADS_PER_PASS, HEADS - GROUP))
         invert_norms(1)
         project(0, range(HEADS - GROUP, HEADS))
-        norms(2)
         turn(0)
-        norms(3)
         prepare_gain()
-        norms(4)
+        norms(2)
         keep_gain()
         for i in range(1, TILES):
             measure_tile(i)
@@ -353,6 +356,8 @@ def tile_block_pb_kernel(tc, attn_out, v, x, wo_words, wo_scales, attn_scale, ou
             project(i, range(HEADS))
             if i < last:
                 turn(i)
+                if i + 2 < TILES:
+                    norms(i + 2)
                 multiply_channels(i - 1)
             else:
                 multiply_tokens(i - 1)

@@ -98,10 +98,10 @@ def tile_block_pb_kernel(tc, attn_out, v, x, wo_words, wo_scales, attn_scale, ou
         load_values(1)
         load_heads(1)
         load_values(2)
+        load_values(3)
         nc.sync.dma_start(out=gain_rows[0 : D // P, :], in_=attn_scale.rearrange("(r c) -> r c", c=P))
         nc.sync.dma_start(out=w_words[:].bitcast(I32), in_=wo_words.bitcast(I32).rearrange("g p w -> p g w"))
         load_heads(2)
-        load_values(3)
         load_heads(3)
         for i in range(TILES):
             load_residual(i)
@@ -133,20 +133,26 @@ def tile_block_pb_kernel(tc, attn_out, v, x, wo_words, wo_scales, attn_scale, ou
         y_tiles, code_tiles, plane_tiles, grouped_tiles = [], [], [], []
         acc_tiles, scaled_tiles, back_tiles = {}, {}, {}
 
-        def norms(i):
-            squares = per_tile.tile([P, KV_HEADS, HD], F32)
-            sumsq = per_tile.tile([P, KV_HEADS], F32)
-            for h in range(KV_HEADS):
-                nc.scalar.activation(
-                    out=squares[:, h, :], in_=v_head(i, h), func=ACT.Square, accum_out=sumsq[:, h : h + 1]
-                )
+        def norms(g):
+            tiles = range(groups[g].start, groups[g].stop)
+            sumsq = consts.tile([P, len(tiles) * KV_HEADS], F32, name="sumsq_%d" % g)
+            for i in tiles:
+                squares = per_tile.tile([P, KV_HEADS, HD], F32)
+                for h in range(KV_HEADS):
+                    column = (i - groups[g].start) * KV_HEADS + h
+                    nc.scalar.activation(
+                        out=squares[:, h, :],
+                        in_=v_head(i, h),
+                        func=ACT.Square,
+                        accum_out=sumsq[:, column : column + 1],
+                    )
             sumsq_tiles.append(sumsq)
 
-        def clamp_norms(i):
-            clamped = per_tile.tile([P, KV_HEADS], F32)
+        def clamp_norms(g):
+            clamped = consts.tile([P, (groups[g].stop - groups[g].start) * KV_HEADS], F32, name="clamped_%d" % g)
             nc.vector.tensor_scalar(
                 out=clamped[:],
-                in0=sumsq_tiles[i][:],
+                in0=sumsq_tiles[g][:],
                 scalar1=MIN_NORM * MIN_NORM,
                 scalar2=-1.0,
                 op0=ALU.max,
@@ -154,10 +160,15 @@ def tile_block_pb_kernel(tc, attn_out, v, x, wo_words, wo_scales, attn_scale, ou
             )
             clamped_tiles.append(clamped)
 
-        def invert_norms(i):
-            neg_inverse = per_tile.tile([P, KV_HEADS], F32)
-            nc.vector.reciprocal(out=neg_inverse[:], in_=clamped_tiles[i][:])
+        def invert_norms(g):
+            neg_inverse = consts.tile([P, (groups[g].stop - groups[g].start) * KV_HEADS], F32, name="neg_inverse_%d" % g)
+            nc.vector.reciprocal(out=neg_inverse[:], in_=clamped_tiles[g][:])
             neg_inverse_tiles.append(neg_inverse)
+
+        def neg_inverse_of(i, h):
+            g = group_of[i]
+            column = (i - groups[g].start) * KV_HEADS + h
+            return neg_inverse_tiles[g][:, column : column + 1]
 
         def measure(i, scalar_of, sums, heads):
             products = per_tile.tile([P, HEADS, HD], F32)
@@ -174,7 +185,7 @@ def tile_block_pb_kernel(tc, attn_out, v, x, wo_words, wo_scales, attn_scale, ou
 
         def measure_tile(i):
             neg_coef = per_tile.tile([P, HEADS], F32)
-            measure(i, lambda h: neg_inverse_tiles[i][:, h : h + 1], neg_coef, range(HEADS))
+            measure(i, lambda h: neg_inverse_of(i, h), neg_coef, range(HEADS))
             neg_coef_tiles.append(neg_coef)
 
         def project(i, heads):
@@ -256,50 +267,52 @@ def tile_block_pb_kernel(tc, attn_out, v, x, wo_words, wo_scales, attn_scale, ou
                 )
             scaled_tiles[i] = scaled
 
-        def turn_back(i):
-            for half in range(HALVES):
-                back = back_psum.tile([P, BANK], F32)
+        def turn_back(i, half):
+            back = back_psum.tile([P, BANK], F32)
+            nc.tensor.matmul(
+                out=back[:],
+                lhsT=ident_bf16[:],
+                rhs=x_tiles[i][:, half * BANK : (half + 1) * BANK],
+                start=True,
+                stop=False,
+            )
+            for j in range(BLOCKS):
                 nc.tensor.matmul(
-                    out=back[:],
-                    lhsT=ident_bf16[:],
-                    rhs=x_tiles[i][:, half * BANK : (half + 1) * BANK],
-                    start=True,
-                    stop=False,
+                    out=back[:, j * P : (j + 1) * P],
+                    lhsT=scaled_tiles[i][:, half * BLOCKS + j, :],
+                    rhs=ident[:],
+                    is_transpose=True,
+                    start=False,
+                    stop=(j == BLOCKS - 1),
                 )
-                for j in range(BLOCKS):
-                    nc.tensor.matmul(
-                        out=back[:, j * P : (j + 1) * P],
-                        lhsT=scaled_tiles[i][:, half * BLOCKS + j, :],
-                        rhs=ident[:],
-                        is_transpose=True,
-                        start=False,
-                        stop=(j == BLOCKS - 1),
-                    )
-                back_tiles[i, half] = back
+            back_tiles[i, half] = back
 
-        def store(i, half, result):
-            nc.sync.dma_start(out=out_rows[:, i, half * BANK : (half + 1) * BANK], in_=result[:])
+        def store(i, cols, result):
+            nc.sync.dma_start(out=out_rows[:, i, cols], in_=result)
 
         def copy_out(i, half):
             result = per_tile.tile([P, BANK], F32, name="result_%d" % half)
             nc.scalar.copy(out=result[:], in_=back_tiles[i, half][:])
-            store(i, half, result)
+            store(i, slice(half * BANK, (half + 1) * BANK), result[:])
 
-        def multiply_tokens(i):
-            for half in range(HALVES):
-                acc = acc_psum.tile([P, BLOCKS, P], F32)
-                flat = acc[:].rearrange("p j t -> p (j t)")
-                for c in range(PASSES):
-                    nc.tensor.matmul_mx(
-                        out=flat,
-                        lhsT=code_tiles[i][:, P * c : P * (c + 1)].bitcast(FP8X4),
-                        lhsT_scale=plane_tiles[i][:, P * c : P * (c + 1)],
-                        rhs=w_words[:, c, 2 * BANK * half : 2 * BANK * (half + 1)].bitcast(FP4X4),
-                        rhs_scale=w_planes[:, c, BANK * half : BANK * (half + 1)],
-                        start=(c == 0),
-                        stop=(c == PASSES - 1),
-                    )
-                acc_tiles[i, half] = flat
+        def finish_channels(i, half):
+            turn_back(i, half)
+            copy_out(i, half)
+
+        def multiply_tokens(i, order):
+            for half, c in order:
+                if c == 0:
+                    acc = acc_psum.tile([P, BLOCKS, P], F32)
+                    acc_tiles[i, half] = acc[:].rearrange("p j t -> p (j t)")
+                nc.tensor.matmul_mx(
+                    out=acc_tiles[i, half],
+                    lhsT=code_tiles[i][:, P * c : P * (c + 1)].bitcast(FP8X4),
+                    lhsT_scale=plane_tiles[i][:, P * c : P * (c + 1)],
+                    rhs=w_words[:, c, 2 * BANK * half : 2 * BANK * (half + 1)].bitcast(FP4X4),
+                    rhs_scale=w_planes[:, c, BANK * half : BANK * (half + 1)],
+                    start=(c == 0),
+                    stop=(c == PASSES - 1),
+                )
 
         def widen_gain(i, half):
             product = per_tile.tile([P, BANK], F32, name="product_%d" % half)
@@ -311,15 +324,19 @@ def tile_block_pb_kernel(tc, attn_out, v, x, wo_words, wo_scales, attn_scale, ou
             )
             scaled_tiles[i, half] = product
 
-        def add_residual(i, half):
+        def add_residual(i, half, pieces):
             result = per_tile.tile([P, BANK], F32, name="result_%d" % half)
-            nc.vector.tensor_tensor(
-                out=result[:],
-                in0=scaled_tiles[i, half][:],
-                in1=x_tiles[i][:, half * BANK : (half + 1) * BANK],
-                op=ALU.add,
-            )
-            store(i, half, result)
+            width = BANK // pieces
+            for piece in range(pieces):
+                cols = slice(piece * width, (piece + 1) * width)
+                wide_cols = slice(half * BANK + cols.start, half * BANK + cols.stop)
+                nc.vector.tensor_tensor(
+                    out=result[:, cols],
+                    in0=scaled_tiles[i, half][:, cols],
+                    in1=x_tiles[i][:, wide_cols],
+                    op=ALU.add,
+                )
+                store(i, wide_cols, result[:, cols])
 
         last = TILES - 1
         norms(0)
@@ -342,40 +359,45 @@ def tile_block_pb_kernel(tc, attn_out, v, x, wo_words, wo_scales, attn_scale, ou
         project(0, range(HEADS_PER_PASS, HEADS - GROUP))
         invert_norms(1)
         project(0, range(HEADS - GROUP, HEADS))
+        norms(2)
         turn(0)
         prepare_gain()
-        norms(2)
+        norms(3)
         keep_gain()
         for i in range(1, TILES):
             measure_tile(i)
-            if i < last:
+            if i < SINGLE_TILES:
                 clamp_norms(i + 1)
             quantise(i - 1)
-            if i < last:
+            if i < SINGLE_TILES:
                 invert_norms(i + 1)
             project(i, range(HEADS))
+            if i == 3:
+                turn_back(1, 0)
             if i < last:
                 turn(i)
-                if i + 2 < TILES:
-                    norms(i + 2)
                 multiply_channels(i - 1)
             else:
-                multiply_tokens(i - 1)
+                multiply_tokens(i - 1, [(half, c) for half in range(HALVES) for c in range(PASSES)])
                 turn(i)
+            if i == 3:
+                copy_out(1, 0)
             if i - 1 < CHANNELS_FIRST:
                 apply_gain(i - 1)
-            if i >= 2:
-                turn_back(i - 2)
-                for half in range(HALVES):
-                    copy_out(i - 2, half)
+            if i == 2:
+                finish_channels(0, 0)
+                finish_channels(0, 1)
+        finish_channels(1, 1)
+        finish_channels(2, 0)
+        finish_channels(2, 1)
         for half in range(HALVES):
             widen_gain(last - 1, half)
         open_codes(last)
         for c in range(PASSES):
             quantise_columns(last, slice(P * c, P * (c + 1)))
-            add_residual(last - 1, c)
-        multiply_tokens(last)
+            multiply_tokens(last, [(half, c) for half in range(HALVES)])
+            add_residual(last - 1, c, 1)
         for half in range(HALVES):
             widen_gain(last, half)
         for half in range(HALVES):
-            add_residual(last, half)
+            add_residual(last, half, 1 + half)

@@ -31,6 +31,7 @@ HALVES = D // BANK
 BLOCKS = BANK // P
 MIN_NORM = 1e-12
 SINGLE_TILES = 3
+SCALAR_SUMS = (1, 2, 3)
 CHANNELS_FIRST = 3
 
 FLOPS = 2 * TOKENS * C * D
@@ -88,8 +89,11 @@ def tile_block_pb_kernel(tc, attn_out, v, x, wo_words, wo_scales, attn_scale, ou
         def load_residual(i):
             nc.sync.dma_start(out=x_tiles[i][:], in_=x_rows[:, i, :])
 
-        load_values(0)
-        load_heads(0)
+        for c in range(PASSES):
+            values = slice(c * KV_HEADS // PASSES, (c + 1) * KV_HEADS // PASSES)
+            heads = slice(c * HEADS_PER_PASS, (c + 1) * HEADS_PER_PASS)
+            nc.sync.dma_start(out=v_loads[0][:, values, :, :], in_=v_rows[:, values, groups[0], :])
+            nc.sync.dma_start(out=a_loads[0][:, heads, :, :], in_=a_rows[:, heads, groups[0], :])
         for q in range(4):
             nc.sync.dma_start(
                 out=w_planes[32 * q : 32 * q + 4, :, :].bitcast(I32),
@@ -108,13 +112,19 @@ def tile_block_pb_kernel(tc, attn_out, v, x, wo_words, wo_scales, attn_scale, ou
         gain_wide = consts.tile([P, D], BF16)
         nc.sync.dma_start(out=gain_wide[:], in_=attn_scale.partition_broadcast(P))
 
-        def v_head(i, h):
+        def v_heads(i):
             g = group_of[i]
-            return v_loads[g][:, h, i - groups[g].start, :]
+            return v_loads[g][:, :, i - groups[g].start, :]
+
+        def a_heads(i):
+            g = group_of[i]
+            return a_loads[g][:, :, i - groups[g].start, :]
+
+        def v_head(i, h):
+            return v_heads(i)[:, h, :]
 
         def a_head(i, hg):
-            g = group_of[i]
-            return a_loads[g][:, hg, i - groups[g].start, :]
+            return a_heads(i)[:, hg, :]
 
         gain = consts.tile([P, D // P], F32)
         gain_turned = []
@@ -122,12 +132,12 @@ def tile_block_pb_kernel(tc, attn_out, v, x, wo_words, wo_scales, attn_scale, ou
         def prepare_gain():
             gain_rows_f32 = consts.tile([P, P], F32)
             nc.scalar.copy(out=gain_rows_f32[:], in_=gain_rows[:])
-            turned = turn_psum.tile([P, 2, P], F32)
-            nc.tensor.transpose(out=turned[:, 0, :], in_=gain_rows_f32[:], identity=ident[:])
-            gain_turned.append(turned)
+            back = back_psum.tile([P, BANK], F32)
+            nc.tensor.transpose(out=back[:, 0:P], in_=gain_rows_f32[:], identity=ident[:])
+            gain_turned.append(back)
 
         def keep_gain():
-            nc.scalar.copy(out=gain[:], in_=gain_turned[0][:, 0, 0 : D // P])
+            nc.scalar.copy(out=gain[:], in_=gain_turned[0][:, 0 : D // P])
 
         sumsq_tiles, clamped_tiles, neg_inverse_tiles, neg_coef_tiles = [], [], [], []
         y_tiles, code_tiles, plane_tiles, grouped_tiles = [], [], [], []
@@ -185,8 +195,31 @@ def tile_block_pb_kernel(tc, attn_out, v, x, wo_words, wo_scales, attn_scale, ou
 
         def measure_tile(i):
             neg_coef = per_tile.tile([P, HEADS], F32)
-            measure(i, lambda h: neg_inverse_of(i, h), neg_coef, range(HEADS))
             neg_coef_tiles.append(neg_coef)
+            if i not in SCALAR_SUMS:
+                measure(i, lambda h: neg_inverse_of(i, h), neg_coef, range(HEADS))
+                return
+            h0 = HEADS_PER_PASS // GROUP
+            half_products = per_tile.tile([P, HEADS_PER_PASS, HD], F32)
+            nc.vector.tensor_tensor(
+                out=half_products[:].rearrange("p (h g) d -> p h g d", g=GROUP),
+                in0=a_heads(i)[:, HEADS_PER_PASS:HEADS, :].rearrange("p (h g) d -> p h g d", g=GROUP),
+                in1=v_heads(i)[:, h0:KV_HEADS, :]
+                .unsqueeze(2)
+                .to_broadcast([P, KV_HEADS - h0, GROUP, HD]),
+                op=ALU.mult,
+            )
+            scaled_products = per_tile.tile([P, HEADS_PER_PASS, HD], F32)
+            for j in range(HEADS_PER_PASS):
+                hg = HEADS_PER_PASS + j
+                nc.scalar.activation(
+                    out=scaled_products[:, j, :],
+                    in_=half_products[:, j, :],
+                    func=ACT.Copy,
+                    scale=neg_inverse_of(i, hg // GROUP),
+                    accum_out=neg_coef[:, hg : hg + 1],
+                )
+            measure(i, lambda h: neg_inverse_of(i, h), neg_coef, range(HEADS_PER_PASS))
 
         def project(i, heads):
             if i == len(y_tiles):
@@ -269,35 +302,33 @@ def tile_block_pb_kernel(tc, attn_out, v, x, wo_words, wo_scales, attn_scale, ou
 
         def turn_back(i, half):
             back = back_psum.tile([P, BANK], F32)
-            nc.tensor.matmul(
-                out=back[:],
-                lhsT=ident_bf16[:],
-                rhs=x_tiles[i][:, half * BANK : (half + 1) * BANK],
-                start=True,
-                stop=False,
-            )
+            with_residual = half == 0
+            if with_residual:
+                nc.tensor.matmul(
+                    out=back[:],
+                    lhsT=ident_bf16[:],
+                    rhs=x_tiles[i][:, half * BANK : (half + 1) * BANK],
+                    start=True,
+                    stop=False,
+                )
             for j in range(BLOCKS):
                 nc.tensor.matmul(
                     out=back[:, j * P : (j + 1) * P],
                     lhsT=scaled_tiles[i][:, half * BLOCKS + j, :],
                     rhs=ident[:],
                     is_transpose=True,
-                    start=False,
-                    stop=(j == BLOCKS - 1),
+                    start=not with_residual,
+                    stop=not with_residual or j == BLOCKS - 1,
                 )
             back_tiles[i, half] = back
 
         def store(i, cols, result):
             nc.sync.dma_start(out=out_rows[:, i, cols], in_=result)
 
-        def copy_out(i, half):
-            result = per_tile.tile([P, BANK], F32, name="result_%d" % half)
-            nc.scalar.copy(out=result[:], in_=back_tiles[i, half][:])
-            store(i, slice(half * BANK, (half + 1) * BANK), result[:])
-
-        def finish_channels(i, half):
-            turn_back(i, half)
-            copy_out(i, half)
+        def copy_out(i):
+            result = per_tile.tile([P, BANK], F32, name="result_0")
+            nc.scalar.copy(out=result[:], in_=back_tiles[i, 0][:])
+            store(i, slice(0, BANK), result[:])
 
         def multiply_tokens(i, order):
             for half, c in order:
@@ -324,7 +355,7 @@ def tile_block_pb_kernel(tc, attn_out, v, x, wo_words, wo_scales, attn_scale, ou
             )
             scaled_tiles[i, half] = product
 
-        def add_residual(i, half, pieces):
+        def add_residual(i, half, summand, pieces=1):
             result = per_tile.tile([P, BANK], F32, name="result_%d" % half)
             width = BANK // pieces
             for piece in range(pieces):
@@ -332,7 +363,7 @@ def tile_block_pb_kernel(tc, attn_out, v, x, wo_words, wo_scales, attn_scale, ou
                 wide_cols = slice(half * BANK + cols.start, half * BANK + cols.stop)
                 nc.vector.tensor_tensor(
                     out=result[:, cols],
-                    in0=scaled_tiles[i, half][:, cols],
+                    in0=summand[:, cols],
                     in1=x_tiles[i][:, wide_cols],
                     op=ALU.add,
                 )
@@ -361,11 +392,19 @@ def tile_block_pb_kernel(tc, attn_out, v, x, wo_words, wo_scales, attn_scale, ou
         project(0, range(HEADS - GROUP, HEADS))
         norms(2)
         turn(0)
-        prepare_gain()
-        norms(3)
-        keep_gain()
         for i in range(1, TILES):
             measure_tile(i)
+            if i == 1:
+                prepare_gain()
+                norms(3)
+                keep_gain()
+            if i == 3:
+                turn_back(0, 0)
+                turn_back(0, 1)
+            if i >= 2:
+                apply_gain(i - 2)
+            if i == 3:
+                copy_out(0)
             if i < SINGLE_TILES:
                 clamp_norms(i + 1)
             quantise(i - 1)
@@ -381,23 +420,22 @@ def tile_block_pb_kernel(tc, attn_out, v, x, wo_words, wo_scales, attn_scale, ou
                 multiply_tokens(i - 1, [(half, c) for half in range(HALVES) for c in range(PASSES)])
                 turn(i)
             if i == 3:
-                copy_out(1, 0)
-            if i - 1 < CHANNELS_FIRST:
-                apply_gain(i - 1)
-            if i == 2:
-                finish_channels(0, 0)
-                finish_channels(0, 1)
-        finish_channels(1, 1)
-        finish_channels(2, 0)
-        finish_channels(2, 1)
+                copy_out(1)
+        turn_back(1, 1)
+        turn_back(2, 0)
+        turn_back(2, 1)
+        copy_out(2)
+        add_residual(0, 1, back_tiles[0, 1])
         for half in range(HALVES):
             widen_gain(last - 1, half)
         open_codes(last)
         for c in range(PASSES):
             quantise_columns(last, slice(P * c, P * (c + 1)))
             multiply_tokens(last, [(half, c) for half in range(HALVES)])
-            add_residual(last - 1, c, 1)
+            add_residual(last - 1, c, scaled_tiles[last - 1, c])
+        for i in (1, 2):
+            add_residual(i, 1, back_tiles[i, 1])
         for half in range(HALVES):
             widen_gain(last, half)
         for half in range(HALVES):
-            add_residual(last, half, 1 + half)
+            add_residual(last, half, scaled_tiles[last, half], pieces=1 + half)

@@ -34,6 +34,8 @@ SINGLE_TILES = 3
 SCALAR_SUMS = (1, 2, 3)
 CHANNELS_FIRST = 3
 
+LAST_BLOCKS = range(2, BLOCKS)
+
 FLOPS = 2 * TOKENS * C * D
 
 
@@ -141,7 +143,7 @@ def tile_block_pb_kernel(tc, attn_out, v, x, wo_words, wo_scales, attn_scale, ou
 
         sumsq_tiles, clamped_tiles, neg_inverse_tiles, neg_coef_tiles = [], [], [], []
         y_tiles, code_tiles, plane_tiles, grouped_tiles = [], [], [], []
-        acc_tiles, scaled_tiles, back_tiles = {}, {}, {}
+        channel_tiles, scaled_tiles, back_tiles, token_tiles, product_tiles = {}, {}, {}, {}, {}
 
         def norms(g):
             tiles = range(groups[g].start, groups[g].stop)
@@ -272,102 +274,97 @@ def tile_block_pb_kernel(tc, attn_out, v, x, wo_words, wo_scales, attn_scale, ou
             open_codes(i)
             quantise_columns(i, slice(0, PASSES * P))
 
-        def multiply_channels(i):
-            for half in range(HALVES):
-                acc = acc_psum.tile([P, BLOCKS, P], F32)
-                for j in range(BLOCKS):
-                    n = half * BLOCKS + j
-                    for c in range(PASSES):
-                        nc.tensor.matmul_mx(
-                            out=acc[:, j, :],
-                            lhsT=w_words[:, c, 2 * P * n : 2 * P * (n + 1)].bitcast(FP4X4),
-                            lhsT_scale=w_planes[:, c, P * n : P * (n + 1)],
-                            rhs=code_tiles[i][:, P * c : P * (c + 1)].bitcast(FP8X4),
-                            rhs_scale=plane_tiles[i][:, P * c : P * (c + 1)],
-                            start=(c == 0),
-                            stop=(c == PASSES - 1),
-                        )
-                acc_tiles[i, half] = acc
+        def multiply_channels(i, half, blocks):
+            acc = acc_psum.tile([P, BLOCKS, P], F32)
+            for j in blocks:
+                n = half * BLOCKS + j
+                for c in range(PASSES):
+                    nc.tensor.matmul_mx(
+                        out=acc[:, j, :],
+                        lhsT=w_words[:, c, 2 * P * n : 2 * P * (n + 1)].bitcast(FP4X4),
+                        lhsT_scale=w_planes[:, c, P * n : P * (n + 1)],
+                        rhs=code_tiles[i][:, P * c : P * (c + 1)].bitcast(FP8X4),
+                        rhs_scale=plane_tiles[i][:, P * c : P * (c + 1)],
+                        start=(c == 0),
+                        stop=(c == PASSES - 1),
+                    )
+            channel_tiles[i, half] = acc
 
-        def apply_gain(i):
-            scaled = per_tile.tile([P, D // P, P], F32)
-            for n in range(D // P):
+        def apply_gain(i, half, blocks):
+            scaled = per_tile.tile([P, BLOCKS, P], F32, name="scaled_%d" % half)
+            for j in blocks:
+                n = half * BLOCKS + j
                 nc.scalar.activation(
-                    out=scaled[:, n, :],
-                    in_=acc_tiles[i, n // BLOCKS][:, n % BLOCKS, :],
+                    out=scaled[:, j, :],
+                    in_=channel_tiles[i, half][:, j, :],
                     func=ACT.Copy,
                     scale=gain[:, n : n + 1],
                 )
-            scaled_tiles[i] = scaled
+            scaled_tiles[i, half] = scaled
 
-        def turn_back(i, half):
+        def turn_back(i, half, blocks, with_residual):
             back = back_psum.tile([P, BANK], F32)
-            with_residual = half == 0
             if with_residual:
+                cols = slice(blocks.start * P, blocks.stop * P)
                 nc.tensor.matmul(
-                    out=back[:],
+                    out=back[:, cols],
                     lhsT=ident_bf16[:],
-                    rhs=x_tiles[i][:, half * BANK : (half + 1) * BANK],
+                    rhs=x_tiles[i][:, half * BANK + cols.start : half * BANK + cols.stop],
                     start=True,
                     stop=False,
                 )
-            for j in range(BLOCKS):
+            for j in blocks:
                 nc.tensor.matmul(
                     out=back[:, j * P : (j + 1) * P],
-                    lhsT=scaled_tiles[i][:, half * BLOCKS + j, :],
+                    lhsT=scaled_tiles[i, half][:, j, :],
                     rhs=ident[:],
                     is_transpose=True,
                     start=not with_residual,
-                    stop=not with_residual or j == BLOCKS - 1,
+                    stop=not with_residual or j == blocks.stop - 1,
                 )
             back_tiles[i, half] = back
 
         def store(i, cols, result):
             nc.sync.dma_start(out=out_rows[:, i, cols], in_=result)
 
-        def copy_out(i):
-            result = per_tile.tile([P, BANK], F32, name="result_0")
-            nc.scalar.copy(out=result[:], in_=back_tiles[i, 0][:])
-            store(i, slice(0, BANK), result[:])
+        def copy_out(i, half, blocks):
+            result = per_tile.tile([P, BANK], F32, name="copied_%d" % half)
+            cols = slice(blocks.start * P, blocks.stop * P)
+            nc.scalar.copy(out=result[:, cols], in_=back_tiles[i, half][:, cols])
+            store(i, slice(half * BANK + cols.start, half * BANK + cols.stop), result[:, cols])
 
-        def multiply_tokens(i, order):
-            for half, c in order:
-                if c == 0:
-                    acc = acc_psum.tile([P, BLOCKS, P], F32)
-                    acc_tiles[i, half] = acc[:].rearrange("p j t -> p (j t)")
+        def multiply_tokens(i, half, cols, passes):
+            if (i, half) not in token_tiles:
+                token_tiles[i, half] = acc_psum.tile([P, BANK], F32, name="acc")
+            first, stop = half * BANK + cols.start, half * BANK + cols.stop
+            for c in passes:
                 nc.tensor.matmul_mx(
-                    out=acc_tiles[i, half],
+                    out=token_tiles[i, half][:, cols],
                     lhsT=code_tiles[i][:, P * c : P * (c + 1)].bitcast(FP8X4),
                     lhsT_scale=plane_tiles[i][:, P * c : P * (c + 1)],
-                    rhs=w_words[:, c, 2 * BANK * half : 2 * BANK * (half + 1)].bitcast(FP4X4),
-                    rhs_scale=w_planes[:, c, BANK * half : BANK * (half + 1)],
+                    rhs=w_words[:, c, 2 * first : 2 * stop].bitcast(FP4X4),
+                    rhs_scale=w_planes[:, c, first:stop],
                     start=(c == 0),
                     stop=(c == PASSES - 1),
                 )
 
-        def widen_gain(i, half):
+        def widen_gain(i, half, cols):
             product = per_tile.tile([P, BANK], F32, name="product_%d" % half)
             nc.vector.tensor_tensor(
-                out=product[:],
-                in0=acc_tiles[i, half],
-                in1=gain_wide[:, half * BANK : (half + 1) * BANK],
+                out=product[:, cols],
+                in0=token_tiles[i, half][:, cols],
+                in1=gain_wide[:, half * BANK + cols.start : half * BANK + cols.stop],
                 op=ALU.mult,
             )
-            scaled_tiles[i, half] = product
+            product_tiles[i, half] = product
 
-        def add_residual(i, half, summand, pieces=1):
+        def add_residual(i, half, cols, summand):
             result = per_tile.tile([P, BANK], F32, name="result_%d" % half)
-            width = BANK // pieces
-            for piece in range(pieces):
-                cols = slice(piece * width, (piece + 1) * width)
-                wide_cols = slice(half * BANK + cols.start, half * BANK + cols.stop)
-                nc.vector.tensor_tensor(
-                    out=result[:, cols],
-                    in0=summand[:, cols],
-                    in1=x_tiles[i][:, wide_cols],
-                    op=ALU.add,
-                )
-                store(i, wide_cols, result[:, cols])
+            wide_cols = slice(half * BANK + cols.start, half * BANK + cols.stop)
+            nc.vector.tensor_tensor(
+                out=result[:, cols], in0=summand[:, cols], in1=x_tiles[i][:, wide_cols], op=ALU.add
+            )
+            store(i, wide_cols, result[:, cols])
 
         last = TILES - 1
         norms(0)
@@ -392,6 +389,7 @@ def tile_block_pb_kernel(tc, attn_out, v, x, wo_words, wo_scales, attn_scale, ou
         project(0, range(HEADS - GROUP, HEADS))
         norms(2)
         turn(0)
+        whole, full = range(BLOCKS), slice(0, BANK)
         for i in range(1, TILES):
             measure_tile(i)
             if i == 1:
@@ -399,12 +397,15 @@ def tile_block_pb_kernel(tc, attn_out, v, x, wo_words, wo_scales, attn_scale, ou
                 norms(3)
                 keep_gain()
             if i == 3:
-                turn_back(0, 0)
-                turn_back(0, 1)
+                turn_back(0, 0, whole, True)
+                turn_back(0, 1, whole, False)
             if i >= 2:
-                apply_gain(i - 2)
+                for half in range(HALVES):
+                    apply_gain(i - 2, half, whole)
             if i == 3:
-                copy_out(0)
+                copy_out(0, 0, whole)
+            if i == last:
+                add_residual(0, 1, full, back_tiles[0, 1])
             if i < SINGLE_TILES:
                 clamp_norms(i + 1)
             quantise(i - 1)
@@ -412,30 +413,40 @@ def tile_block_pb_kernel(tc, attn_out, v, x, wo_words, wo_scales, attn_scale, ou
                 invert_norms(i + 1)
             project(i, range(HEADS))
             if i == 3:
-                turn_back(1, 0)
+                turn_back(1, 0, whole, True)
             if i < last:
                 turn(i)
-                multiply_channels(i - 1)
+                for half in range(HALVES):
+                    multiply_channels(i - 1, half, whole)
             else:
-                multiply_tokens(i - 1, [(half, c) for half in range(HALVES) for c in range(PASSES)])
+                for half in range(HALVES):
+                    multiply_tokens(i - 1, half, full, range(PASSES))
                 turn(i)
             if i == 3:
-                copy_out(1)
-        turn_back(1, 1)
-        turn_back(2, 0)
-        turn_back(2, 1)
-        copy_out(2)
-        add_residual(0, 1, back_tiles[0, 1])
+                copy_out(1, 0, whole)
+        turn_back(1, 1, whole, False)
+        turn_back(2, 0, whole, True)
+        turn_back(2, 1, whole, False)
         for half in range(HALVES):
-            widen_gain(last - 1, half)
+            widen_gain(last - 1, half, full)
         open_codes(last)
-        for c in range(PASSES):
-            quantise_columns(last, slice(P * c, P * (c + 1)))
-            multiply_tokens(last, [(half, c) for half in range(HALVES)])
-            add_residual(last - 1, c, scaled_tiles[last - 1, c])
+        quantise_columns(last, slice(0, P))
+        multiply_tokens(last, 0, full, range(0, 1))
+        add_residual(last - 1, 0, full, product_tiles[last - 1, 0])
+        copy_out(2, 0, whole)
+        quantise_columns(last, slice(P, 2 * P))
+        multiply_tokens(last, 0, full, range(1, PASSES))
+        multiply_channels(last, 1, LAST_BLOCKS)
+        for j in range(LAST_BLOCKS.start):
+            multiply_tokens(last, 1, slice(j * P, (j + 1) * P), range(PASSES))
+        apply_gain(last, 1, LAST_BLOCKS)
+        turn_back(last, 1, LAST_BLOCKS, True)
+        add_residual(last - 1, 1, full, product_tiles[last - 1, 1])
         for i in (1, 2):
-            add_residual(i, 1, back_tiles[i, 1])
-        for half in range(HALVES):
-            widen_gain(last, half)
-        for half in range(HALVES):
-            add_residual(last, half, scaled_tiles[last, half], pieces=1 + half)
+            add_residual(i, 1, full, back_tiles[i, 1])
+        tokens_cols = slice(0, LAST_BLOCKS.start * P)
+        widen_gain(last, 0, full)
+        widen_gain(last, 1, tokens_cols)
+        add_residual(last, 0, full, product_tiles[last, 0])
+        copy_out(last, 1, LAST_BLOCKS)
+        add_residual(last, 1, tokens_cols, product_tiles[last, 1])

from contextlib import ExitStack

import concourse.mybir as mybir
from concourse.masks import make_identity

BF16 = mybir.dt.bfloat16
F32 = mybir.dt.float32
I32 = mybir.dt.int32
U32 = mybir.dt.uint32
U8 = mybir.dt.uint8
FP8X4 = mybir.dt.float8_e4m3fn_x4
FP4X4 = mybir.dt.float4_e2m1fn_x4
ALU = mybir.AluOpType
ACT = mybir.ActivationFunctionType

P = 128
TOKENS = 640
TILES = TOKENS // P
KV_HEADS = 4
GROUP = 2
HEADS = KV_HEADS * GROUP
HD = 128
C = HEADS * HD
D = 1024
PACK = 4
K_PASS = P * PACK
PASSES = C // K_PASS
HEADS_PER_PASS = K_PASS // HD
BANK = 512
HALVES = D // BANK
BLOCKS = BANK // P
MIN_NORM = 1e-12
SINGLE_TILES = 3
SCALAR_SUMS = (1, 2, 3)
CHANNELS_FIRST = 3

LAST_BLOCKS = range(2, BLOCKS)

FLOPS = 2 * TOKENS * C * D


def tile_block_pb_kernel(tc, attn_out, v, x, wo_words, wo_scales, attn_scale, out):
    nc = tc.nc
    a_rows = attn_out.rearrange("b h g (p i) d -> p (b h g) i d", i=TILES)
    v_rows = v.rearrange("b h (p i) d -> p (b h) i d", i=TILES)
    x_rows = x.rearrange("b (p i) n -> p (b i) n", i=TILES)
    out_rows = out.rearrange("b (p i) n -> p (b i) n", i=TILES)

    with ExitStack() as ctx:
        consts = ctx.enter_context(tc.tile_pool(name="consts", bufs=1))
        per_tile = ctx.enter_context(tc.tile_pool(name="per_tile", bufs=TILES))
        turn_psum = ctx.enter_context(tc.psum_pool(name="turn_psum", bufs=2))
        acc_psum = ctx.enter_context(tc.psum_pool(name="acc_psum", bufs=3))
        back_psum = ctx.enter_context(tc.psum_pool(name="back_psum", bufs=3))
        ctx.enter_context(tc.manual_schedule())

        ident = consts.tile([P, P], F32)
        make_identity(nc, ident[:])
        ident_bf16 = consts.tile([P, P], BF16)
        nc.gpsimd.tensor_copy(out=ident_bf16[:], in_=ident[:])
        gain_rows = consts.tile([P, P], BF16)
        nc.vector.memset(gain_rows[:], 0.0)
        w_planes = consts.tile([P, PASSES, D], U8, align_bytes=64)
        nc.vector.memset(w_planes[:].bitcast(I32), 0)
        w_words = consts.tile([P, PASSES, 2 * D], U8, align_bytes=64)
        seed = consts.tile([P, 1], F32)
        nc.vector.memset(seed[:], 0.0)
        seed_squared = consts.tile([P, 1], F32)
        nc.scalar.activation(out=seed_squared[:], in_=seed[:], func=ACT.Square)

        groups = [slice(i, i + 1) for i in range(SINGLE_TILES)] + [slice(SINGLE_TILES, TILES)]
        group_of = [g for g, tiles in enumerate(groups) for i in range(tiles.start, tiles.stop)]
        v_loads = [
            consts.tile([P, KV_HEADS, tiles.stop - tiles.start, HD], BF16, name="v_%d" % tiles.start)
            for tiles in groups
        ]
        a_loads = [
            consts.tile([P, HEADS, tiles.stop - tiles.start, HD], BF16, name="a_%d" % tiles.start)
            for tiles in groups
        ]
        x_tiles = [consts.tile([P, D], BF16, name="x_%d" % i) for i in range(TILES)]

        def load_values(g):
            nc.sync.dma_start(out=v_loads[g][:], in_=v_rows[:, :, groups[g], :])

        def load_heads(g):
            for c in range(PASSES):
                heads = slice(c * HEADS_PER_PASS, (c + 1) * HEADS_PER_PASS)
                nc.sync.dma_start(out=a_loads[g][:, heads, :, :], in_=a_rows[:, heads, groups[g], :])

        def load_residual(i):
            nc.sync.dma_start(out=x_tiles[i][:], in_=x_rows[:, i, :])

        for c in range(PASSES):
            values = slice(c * KV_HEADS // PASSES, (c + 1) * KV_HEADS // PASSES)
            heads = slice(c * HEADS_PER_PASS, (c + 1) * HEADS_PER_PASS)
            nc.sync.dma_start(out=v_loads[0][:, values, :, :], in_=v_rows[:, values, groups[0], :])
            nc.sync.dma_start(out=a_loads[0][:, heads, :, :], in_=a_rows[:, heads, groups[0], :])
        for q in range(4):
            nc.sync.dma_start(
                out=w_planes[32 * q : 32 * q + 4, :, :].bitcast(I32),
                in_=wo_scales.bitcast(I32)[:, 4 * q : 4 * q + 4, :].rearrange("g r n -> r g n"),
            )
        load_values(1)
        load_heads(1)
        load_values(2)
        load_values(3)
        nc.sync.dma_start(out=gain_rows[0 : D // P, :], in_=attn_scale.rearrange("(r c) -> r c", c=P))
        nc.sync.dma_start(out=w_words[:].bitcast(I32), in_=wo_words.bitcast(I32).rearrange("g p w -> p g w"))
        load_heads(2)
        load_heads(3)
        for i in range(TILES):
            load_residual(i)
        gain_wide = consts.tile([P, D], BF16)
        nc.sync.dma_start(out=gain_wide[:], in_=attn_scale.partition_broadcast(P))

        def v_heads(i):
            g = group_of[i]
            return v_loads[g][:, :, i - groups[g].start, :]

        def a_heads(i):
            g = group_of[i]
            return a_loads[g][:, :, i - groups[g].start, :]

        def v_head(i, h):
            return v_heads(i)[:, h, :]

        def a_head(i, hg):
            return a_heads(i)[:, hg, :]

        gain = consts.tile([P, D // P], F32)
        gain_turned = []

        def prepare_gain():
            gain_rows_f32 = consts.tile([P, P], F32)
            nc.scalar.copy(out=gain_rows_f32[:], in_=gain_rows[:])
            back = back_psum.tile([P, BANK], F32)
            nc.tensor.transpose(out=back[:, 0:P], in_=gain_rows_f32[:], identity=ident[:])
            gain_turned.append(back)

        def keep_gain():
            nc.scalar.copy(out=gain[:], in_=gain_turned[0][:, 0 : D // P])

        sumsq_tiles, clamped_tiles, neg_inverse_tiles, neg_coef_tiles = [], [], [], []
        y_tiles, code_tiles, plane_tiles, grouped_tiles = [], [], [], []
        channel_tiles, scaled_tiles, back_tiles, token_tiles, product_tiles = {}, {}, {}, {}, {}

        def norms(g):
            tiles = range(groups[g].start, groups[g].stop)
            sumsq = consts.tile([P, len(tiles) * KV_HEADS], F32, name="sumsq_%d" % g)
            for i in tiles:
                squares = per_tile.tile([P, KV_HEADS, HD], F32)
                for h in range(KV_HEADS):
                    column = (i - groups[g].start) * KV_HEADS + h
                    nc.scalar.activation(
                        out=squares[:, h, :],
                        in_=v_head(i, h),
                        func=ACT.Square,
                        accum_out=sumsq[:, column : column + 1],
                    )
            sumsq_tiles.append(sumsq)

        def clamp_norms(g):
            clamped = consts.tile([P, (groups[g].stop - groups[g].start) * KV_HEADS], F32, name="clamped_%d" % g)
            nc.vector.tensor_scalar(
                out=clamped[:],
                in0=sumsq_tiles[g][:],
                scalar1=MIN_NORM * MIN_NORM,
                scalar2=-1.0,
                op0=ALU.max,
                op1=ALU.mult,
            )
            clamped_tiles.append(clamped)

        def invert_norms(g):
            neg_inverse = consts.tile([P, (groups[g].stop - groups[g].start) * KV_HEADS], F32, name="neg_inverse_%d" % g)
            nc.vector.reciprocal(out=neg_inverse[:], in_=clamped_tiles[g][:])
            neg_inverse_tiles.append(neg_inverse)

        def neg_inverse_of(i, h):
            g = group_of[i]
            column = (i - groups[g].start) * KV_HEADS + h
            return neg_inverse_tiles[g][:, column : column + 1]

        def measure(i, scalar_of, sums, heads):
            products = per_tile.tile([P, HEADS, HD], F32)
            for hg in heads:
                nc.vector.scalar_tensor_tensor(
                    out=products[:, hg, :],
                    in0=a_head(i, hg),
                    scalar=scalar_of(hg // GROUP),
                    in1=v_head(i, hg // GROUP),
                    op0=ALU.mult,
                    op1=ALU.mult,
                    accum_out=sums[:, hg : hg + 1],
                )

        def measure_tile(i):
            neg_coef = per_tile.tile([P, HEADS], F32)
            neg_coef_tiles.append(neg_coef)
            if i not in SCALAR_SUMS:
                measure(i, lambda h: neg_inverse_of(i, h), neg_coef, range(HEADS))
                return
            h0 = HEADS_PER_PASS // GROUP
            half_products = per_tile.tile([P, HEADS_PER_PASS, HD], F32)
            nc.vector.tensor_tensor(
                out=half_products[:].rearrange("p (h g) d -> p h g d", g=GROUP),
                in0=a_heads(i)[:, HEADS_PER_PASS:HEADS, :].rearrange("p (h g) d -> p h g d", g=GROUP),
                in1=v_heads(i)[:, h0:KV_HEADS, :]
                .unsqueeze(2)
                .to_broadcast([P, KV_HEADS - h0, GROUP, HD]),
                op=ALU.mult,
            )
            scaled_products = per_tile.tile([P, HEADS_PER_PASS, HD], F32)
            for j in range(HEADS_PER_PASS):
                hg = HEADS_PER_PASS + j
                nc.scalar.activation(
                    out=scaled_products[:, j, :],
                    in_=half_products[:, j, :],
                    func=ACT.Copy,
                    scale=neg_inverse_of(i, hg // GROUP),
                    accum_out=neg_coef[:, hg : hg + 1],
                )
            measure(i, lambda h: neg_inverse_of(i, h), neg_coef, range(HEADS_PER_PASS))

        def project(i, heads):
            if i == len(y_tiles):
                y = per_tile.tile([P, C], BF16)
                y_tiles.append(y)
            y = y_tiles[i]
            for hg in heads:
                nc.vector.scalar_tensor_tensor(
                    out=y[:, hg * HD : (hg + 1) * HD],
                    in0=v_head(i, hg // GROUP),
                    scalar=neg_coef_tiles[i][:, hg : hg + 1],
                    in1=a_head(i, hg),
                    op0=ALU.mult,
                    op1=ALU.add,
                )

        def turn(i):
            y_words = y_tiles[i][:].bitcast(F32)
            words_per_pass = K_PASS // 2
            turned_tiles = []
            for c in range(PASSES):
                turned = turn_psum.tile([P, 2, P], F32)
                for u in range(2):
                    nc.tensor.transpose(
                        out=turned[:, u, :],
                        in_=y_words[:, words_per_pass * c + u : words_per_pass * (c + 1) : 2],
                        identity=ident[:],
                    )
                turned_tiles.append(turned)
            grouped = per_tile.tile([P, C], BF16, align_bytes=64)
            grouped_words = grouped[:].bitcast(F32).rearrange("p (c t u) -> p c t u", c=PASSES, u=2)
            for c in range(PASSES):
                nc.scalar.copy(out=grouped_words[:, c, :, :], in_=turned_tiles[c][:].rearrange("p u t -> p t u"))
            grouped_tiles.append(grouped)

        def quantise_columns(i, cols):
            nc.vector.quantize_mx(
                out=code_tiles[i][:, cols].bitcast(FP8X4),
                scales=plane_tiles[i][:, cols],
                in_=grouped_tiles[i][:, PACK * cols.start : PACK * cols.stop],
            )

        def open_codes(i):
            codes = per_tile.tile([P, PASSES * P], U32, align_bytes=64)
            planes = per_tile.tile([P, PASSES * P], U8, align_bytes=64)
            code_tiles.append(codes)
            plane_tiles.append(planes)

        def quantise(i):
            open_codes(i)
            quantise_columns(i, slice(0, PASSES * P))

        def multiply_channels(i, half, blocks):
            acc = acc_psum.tile([P, BLOCKS, P], F32)
            for j in blocks:
                n = half * BLOCKS + j
                for c in range(PASSES):
                    nc.tensor.matmul_mx(
                        out=acc[:, j, :],
                        lhsT=w_words[:, c, 2 * P * n : 2 * P * (n + 1)].bitcast(FP4X4),
                        lhsT_scale=w_planes[:, c, P * n : P * (n + 1)],
                        rhs=code_tiles[i][:, P * c : P * (c + 1)].bitcast(FP8X4),
                        rhs_scale=plane_tiles[i][:, P * c : P * (c + 1)],
                        start=(c == 0),
                        stop=(c == PASSES - 1),
                    )
            channel_tiles[i, half] = acc

        def apply_gain(i, half, blocks):
            scaled = per_tile.tile([P, BLOCKS, P], F32, name="scaled_%d" % half)
            for j in blocks:
                n = half * BLOCKS + j
                nc.scalar.activation(
                    out=scaled[:, j, :],
                    in_=channel_tiles[i, half][:, j, :],
                    func=ACT.Copy,
                    scale=gain[:, n : n + 1],
                )
            scaled_tiles[i, half] = scaled

        def turn_back(i, half, blocks, with_residual):
            back = back_psum.tile([P, BANK], F32)
            if with_residual:
                cols = slice(blocks.start * P, blocks.stop * P)
                nc.tensor.matmul(
                    out=back[:, cols],
                    lhsT=ident_bf16[:],
                    rhs=x_tiles[i][:, half * BANK + cols.start : half * BANK + cols.stop],
                    start=True,
                    stop=False,
                )
            for j in blocks:
                nc.tensor.matmul(
                    out=back[:, j * P : (j + 1) * P],
                    lhsT=scaled_tiles[i, half][:, j, :],
                    rhs=ident[:],
                    is_transpose=True,
                    start=not with_residual,
                    stop=not with_residual or j == blocks.stop - 1,
                )
            back_tiles[i, half] = back

        def store(i, cols, result):
            nc.sync.dma_start(out=out_rows[:, i, cols], in_=result)

        def copy_out(i, half, blocks):
            result = per_tile.tile([P, BANK], F32, name="copied_%d" % half)
            cols = slice(blocks.start * P, blocks.stop * P)
            nc.scalar.copy(out=result[:, cols], in_=back_tiles[i, half][:, cols])
            store(i, slice(half * BANK + cols.start, half * BANK + cols.stop), result[:, cols])

        def multiply_tokens(i, half, cols, passes):
            if (i, half) not in token_tiles:
                token_tiles[i, half] = acc_psum.tile([P, BANK], F32, name="acc")
            first, stop = half * BANK + cols.start, half * BANK + cols.stop
            for c in passes:
                nc.tensor.matmul_mx(
                    out=token_tiles[i, half][:, cols],
                    lhsT=code_tiles[i][:, P * c : P * (c + 1)].bitcast(FP8X4),
                    lhsT_scale=plane_tiles[i][:, P * c : P * (c + 1)],
                    rhs=w_words[:, c, 2 * first : 2 * stop].bitcast(FP4X4),
                    rhs_scale=w_planes[:, c, first:stop],
                    start=(c == 0),
                    stop=(c == PASSES - 1),
                )

        def widen_gain(i, half, cols):
            product = per_tile.tile([P, BANK], F32, name="product_%d" % half)
            nc.vector.tensor_tensor(
                out=product[:, cols],
                in0=token_tiles[i, half][:, cols],
                in1=gain_wide[:, half * BANK + cols.start : half * BANK + cols.stop],
                op=ALU.mult,
            )
            product_tiles[i, half] = product

        def add_residual(i, half, cols, summand):
            result = per_tile.tile([P, BANK], F32, name="result_%d" % half)
            wide_cols = slice(half * BANK + cols.start, half * BANK + cols.stop)
            nc.vector.tensor_tensor(
                out=result[:, cols], in0=summand[:, cols], in1=x_tiles[i][:, wide_cols], op=ALU.add
            )
            store(i, wide_cols, result[:, cols])

        last = TILES - 1
        norms(0)
        dots = consts.tile([P, HEADS], F32)
        measure(0, lambda h: 1.0, dots, range(HEADS - GROUP))
        clamp_norms(0)
        measure(0, lambda h: 1.0, dots, range(HEADS - GROUP, HEADS))
        invert_norms(0)
        first_coef = per_tile.tile([P, HEADS], F32, name="neg_coef")
        nc.vector.tensor_tensor(
            out=first_coef[:].rearrange("p (h g) -> p h g", g=GROUP),
            in0=dots[:].rearrange("p (h g) -> p h g", g=GROUP),
            in1=neg_inverse_tiles[0][:].unsqueeze(2).to_broadcast([P, KV_HEADS, GROUP]),
            op=ALU.mult,
        )
        neg_coef_tiles.append(first_coef)
        norms(1)
        project(0, range(HEADS_PER_PASS))
        clamp_norms(1)
        project(0, range(HEADS_PER_PASS, HEADS - GROUP))
        invert_norms(1)
        project(0, range(HEADS - GROUP, HEADS))
        norms(2)
        turn(0)
        whole, full = range(BLOCKS), slice(0, BANK)
        for i in range(1, TILES):
            measure_tile(i)
            if i == 1:
                prepare_gain()
                norms(3)
                keep_gain()
            if i == 3:
                turn_back(0, 0, whole, True)
                turn_back(0, 1, whole, False)
            if i >= 2:
                for half in range(HALVES):
                    apply_gain(i - 2, half, whole)
            if i == 3:
                copy_out(0, 0, whole)
            if i == last:
                add_residual(0, 1, full, back_tiles[0, 1])
            if i < SINGLE_TILES:
                clamp_norms(i + 1)
            quantise(i - 1)
            if i < SINGLE_TILES:
                invert_norms(i + 1)
            project(i, range(HEADS))
            if i == 3:
                turn_back(1, 0, whole, True)
            if i < last:
                turn(i)
                for half in range(HALVES):
                    multiply_channels(i - 1, half, whole)
            else:
                for half in range(HALVES):
                    multiply_tokens(i - 1, half, full, range(PASSES))
                turn(i)
            if i == 3:
                copy_out(1, 0, whole)
        turn_back(1, 1, whole, False)
        turn_back(2, 0, whole, True)
        turn_back(2, 1, whole, False)
        for half in range(HALVES):
            widen_gain(last - 1, half, full)
        open_codes(last)
        quantise_columns(last, slice(0, P))
        multiply_tokens(last, 0, full, range(0, 1))
        add_residual(last - 1, 0, full, product_tiles[last - 1, 0])
        copy_out(2, 0, whole)
        quantise_columns(last, slice(P, 2 * P))
        multiply_tokens(last, 0, full, range(1, PASSES))
        multiply_channels(last, 1, LAST_BLOCKS)
        for j in range(LAST_BLOCKS.start):
            multiply_tokens(last, 1, slice(j * P, (j + 1) * P), range(PASSES))
        apply_gain(last, 1, LAST_BLOCKS)
        turn_back(last, 1, LAST_BLOCKS, True)
        add_residual(last - 1, 1, full, product_tiles[last - 1, 1])
        for i in (1, 2):
            add_residual(i, 1, full, back_tiles[i, 1])
        tokens_cols = slice(0, LAST_BLOCKS.start * P)
        widen_gain(last, 0, full)
        widen_gain(last, 1, tokens_cols)
        add_residual(last, 0, full, product_tiles[last, 0])
        copy_out(last, 1, LAST_BLOCKS)
        add_residual(last, 1, tokens_cols, product_tiles[last, 1])
